import numpy as np
import ml_dtypes


def mxq(x, axis, fmt="e4m3"):
    dtype, down = {"e4m3": (ml_dtypes.float8_e4m3fn, 7), "e5m2": (ml_dtypes.float8_e5m2, 14)}[fmt]
    v = np.moveaxis(np.asarray(x, np.float32).astype(ml_dtypes.bfloat16).astype(np.float64), axis, -1)
    blocks = v.reshape(v.shape[:-1] + (-1, 32))
    amax = np.abs(blocks).max(-1, keepdims=True)
    byte = np.maximum(np.where(amax > 0, np.frexp(amax)[1] - 1 + 127, 0) - down, 1)
    scale = np.exp2(byte - 127.0)
    codes = (blocks / scale).astype(np.float32).astype(dtype).astype(np.float64)
    return np.moveaxis((codes * scale).reshape(v.shape), -1, axis)


WIDE = False


def mx_kscale(k):
    if not WIDE:
        return np.ones(k)
    levels = np.array([10, -10, 5, -5, 0])
    if k % 512:
        return np.exp2(np.random.permutation(np.resize(levels, k // 32))).repeat(32)
    a = np.empty((k // 512, 16))
    for p in range(k // 512):
        a[p, :8] = np.random.permutation(np.resize(levels, 8))
        for g in range(8):
            far = levels[np.abs(levels - a[p, g]) >= 10]
            a[p, g + 8] = far[np.random.randint(len(far))]
    return np.exp2(a.ravel()).repeat(32)


BF16 = ml_dtypes.bfloat16


def bf(x):
    return np.asarray(x, np.float32).astype(BF16)


def f64(x):
    return np.asarray(x).astype(np.float64)


N, S, K, Yd, Xd = 256, 4, 16, 512, 512
LOG_2PI = np.log(2.0 * np.pi)


def softplus(v):
    return np.maximum(v, 0.0) + np.log(1.0 + np.exp(-np.abs(v)))


def log_softmax(v, axis):
    m = v - v.max(axis, keepdims=True)
    return m - np.log(np.exp(m).sum(axis, keepdims=True))


def mv_gaussian_log_prob(value, mu, sig_diags, event_shape):
    diff = value - mu
    M = np.sum((diff / sig_diags) ** 2, axis=-1)
    half_log_det = np.sum(np.log(sig_diags), axis=-1)
    return -0.5 * (event_shape * LOG_2PI + M) - half_log_det


def setup_inputs():
    s = mx_kscale(Yd)
    return {"Y": bf(np.random.standard_normal((N, Yd)) * 0.5 * s),
            "We_mu": bf(np.random.standard_normal((Yd, Xd)) * 2.0 / np.sqrt(Yd) / s[:, None]),
            "be_mu": bf(np.random.standard_normal(Xd) * 0.1),
            "We_sig": bf(np.random.standard_normal((Yd, Xd)) * 1.0 / np.sqrt(Yd) / s[:, None]),
            "be_sig": bf(-3.0 + np.random.standard_normal(Xd) * 0.1),
            "phi_mus": bf(np.random.standard_normal((K, Xd)) * 3.0 / np.sqrt(Xd)),
            "phi_sigs": bf(1.0 + (np.random.random_sample((K, Xd)) - 0.5) * 9.0 / np.sqrt(Xd)),
            "phi_logits": bf(np.random.standard_normal(K))}


def reference(Y, We_mu, be_mu, We_sig, be_sig, phi_mus, phi_sigs, phi_logits):
    Yq = mxq(f64(Y), 1, "e4m3")
    enc_mu = (Yq @ mxq(f64(We_mu), 0, "e4m3")) + f64(be_mu)
    enc_sig = softplus((Yq @ mxq(f64(We_sig), 0, "e4m3")) + f64(be_sig)) + 1e-3
    log_pi = log_softmax(f64(phi_logits), -1)
    std_k = enc_sig[:, None, :] + f64(phi_sigs)[None, :, :]
    z_logits = log_pi[None, :] + mv_gaussian_log_prob(enc_mu[:, None, :], f64(phi_mus)[None, :, :], std_k, Xd)
    z_log_probs = log_softmax(z_logits, -1)
    return enc_mu, enc_sig, z_log_probs

@@ -1,0 +1,341 @@
+from contextlib import ExitStack
+
+import concourse.masks as masks
+import concourse.mybir as mybir
+
+F32 = mybir.dt.float32
+BF16 = mybir.dt.bfloat16
+U32 = mybir.dt.uint32
+U8 = mybir.dt.uint8
+FP8X4 = mybir.dt.float8_e4m3fn_x4
+ACT = mybir.ActivationFunctionType
+ALU = mybir.AluOpType
+AXIS = mybir.AxisListType
+
+P = 128
+PSUM_BANKS = 8
+BANK_F32 = 512
+
+ROWS = 256
+Y_DIM = 512
+X_DIM = 512
+CLUSTERS = 16
+SIG_FLOOR = 1e-3
+NT = ROWS // P
+DT = X_DIM // P
+
+PACK = 4
+PAIR = 2
+WORDS = PACK // PAIR
+assert Y_DIM == P * PACK
+RUN = 4
+TILES_PER_BANK = BANK_F32 // ROWS
+
+ROW_PHI_MU = 0
+ROW_PHI_SIG = CLUSTERS
+ROW_BE_MU = 2 * CLUSTERS
+ROW_BE_SIG = 2 * CLUSTERS + 1
+PARAM_ROWS = 2 * CLUSTERS + 2
+
+VECTOR_CLUSTERS = 8
+SCALAR_CLUSTERS = 4
+UNIT_TILES = DT // 2
+UNITS_PER_CLUSTER = DT // UNIT_TILES
+VECTOR_UNITS = VECTOR_CLUSTERS * UNITS_PER_CLUSTER
+GPSIMD_FIRST_UNIT = (VECTOR_CLUSTERS + SCALAR_CLUSTERS) * UNITS_PER_CLUSTER
+ALL_UNITS = CLUSTERS * UNITS_PER_CLUSTER
+VECTOR_START = PSUM_BANKS // NT
+VECTOR_REST = VECTOR_UNITS - (CLUSTERS - VECTOR_START)
+SCALAR_BLOCKS = SCALAR_CLUSTERS * DT
+SCALAR_LEAD = SCALAR_BLOCKS // 2
+
+FLOPS = 2 * 2 * ROWS * Y_DIM * X_DIM
+
+
+def tile_deepgmm_pa_s_kernel(
+    tc, Y, We_mu, be_mu, We_sig, be_sig, phi_mus, phi_sigs, phi_logits, out_0, out_1, out_2
+):
+    nc = tc.nc
+    with ExitStack() as ctx:
+        keep = ctx.enter_context(tc.tile_pool(name="keep", bufs=1))
+        psum = ctx.enter_context(tc.psum_pool(name="psum", bufs=PSUM_BANKS))
+        ctx.enter_context(tc.manual_schedule())
+
+        def load_weight(raw, w):
+            nc.sync.dma_start(out=raw[:], in_=w.rearrange("(p t) c -> p t c", t=PACK))
+
+        def group(grouped, raw):
+            nc.vector.tensor_copy(
+                out=grouped[:].rearrange("p (c i) t -> p c t i", i=RUN),
+                in_=raw[:].rearrange("p t (c i) -> p c t i", i=RUN),
+            )
+
+        def quantise(codes, scales, grouped):
+            nc.vector.quantize_mx(
+                out=codes[:].bitcast(FP8X4),
+                scales=scales[:],
+                in_=grouped[:].rearrange("p c t -> p (c t)"),
+            )
+
+        ident = keep.tile([P, P], F32)
+        masks.make_identity(nc, ident[:])
+        one_col = keep.tile([P, 1], F32)
+        nc.vector.memset(one_col[:], 1.0)
+
+        y_codes = keep.tile([P, ROWS], U32, align_bytes=64)
+        y_scales = keep.tile([P, ROWS], U8, align_bytes=64)
+        wsig_codes = keep.tile([P, X_DIM], U32, align_bytes=64)
+        wsig_scales = keep.tile([P, X_DIM], U8, align_bytes=64)
+        wmu_raw = keep.tile([P, PACK, X_DIM], BF16)
+        logits = keep.tile([P, CLUSTERS], BF16)
+        params = keep.tile([P, DT, PARAM_ROWS], F32)
+
+        with tc.tile_pool(name="early", bufs=1) as early:
+            param_rows = early.tile([P, X_DIM], BF16)
+            nc.vector.memset(param_rows[:], 0.0)
+
+            y_sb = early.tile([P, NT, Y_DIM], BF16)
+            nc.sync.dma_start(out=y_sb[:], in_=Y.rearrange("(t p) k -> p t k", p=P))
+            wsig_raw = early.tile([P, PACK, X_DIM], BF16)
+            load_weight(wsig_raw, We_sig)
+            load_weight(wmu_raw, We_mu)
+            nc.sync.dma_start(out=logits[:], in_=phi_logits.partition_broadcast(P))
+
+            nc.scalar.dma_start(
+                out=param_rows[ROW_PHI_SIG : ROW_PHI_SIG + CLUSTERS, :], in_=phi_sigs
+            )
+            nc.scalar.dma_start(out=param_rows[ROW_PHI_MU : ROW_PHI_MU + CLUSTERS, :], in_=phi_mus)
+            nc.scalar.dma_start(
+                out=param_rows[ROW_BE_SIG : ROW_BE_SIG + 1, :],
+                in_=be_sig.rearrange("(o d) -> o d", o=1),
+            )
+            nc.scalar.dma_start(
+                out=param_rows[ROW_BE_MU : ROW_BE_MU + 1, :],
+                in_=be_mu.rearrange("(o d) -> o d", o=1),
+            )
+
+            warm = keep.tile([P, 1], F32)
+            nc.scalar.activation(out=warm[:], in_=one_col[:], func=ACT.Exp)
+
+            y_words = y_sb[:].bitcast(F32)
+            yT_ps = psum.tile([P, WORDS, ROWS], F32, tag="bank")
+            for nt in range(NT):
+                for u in range(WORDS):
+                    nc.tensor.transpose(
+                        yT_ps[:, u, nt * P : (nt + 1) * P],
+                        y_words[:, nt, u : WORDS * P : WORDS],
+                        ident[:],
+                    )
+            y_grouped = early.tile([P, ROWS, PACK], BF16, align_bytes=64)
+            nc.vector.tensor_copy(
+                out=y_grouped[:].bitcast(F32), in_=yT_ps[:].rearrange("p u n -> p n u")
+            )
+
+            param_rows_f = early.tile([P, X_DIM], F32)
+            nc.scalar.copy(out=param_rows_f[:], in_=param_rows[:])
+            param_ps = psum.tile([P, DT, P], F32, tag="bank")
+            for dt in range(DT):
+                nc.tensor.transpose(
+                    param_ps[:, dt, :], param_rows_f[:, dt * P : (dt + 1) * P], ident[:]
+                )
+            nc.scalar.copy(out=params[:], in_=param_ps[:, :, 0:PARAM_ROWS])
+
+            wsig_grouped = early.tile([P, X_DIM, PACK], BF16, align_bytes=64)
+            group(wsig_grouped, wsig_raw)
+            quantise(y_codes, y_scales, y_grouped)
+            quantise(wsig_codes, wsig_scales, wsig_grouped)
+
+        work = ctx.enter_context(tc.tile_pool(name="work", bufs=3))
+        outs = ctx.enter_context(tc.tile_pool(name="outs", bufs=2 * NT))
+        diffs = ctx.enter_context(tc.tile_pool(name="diffs", bufs=VECTOR_REST))
+
+        def param(dt, row):
+            return params[:, dt, row : row + 1]
+
+        wmu_grouped = keep.tile([P, X_DIM, PACK], BF16, align_bytes=64)
+        group(wmu_grouped, wmu_raw)
+
+        def project(w_codes, w_scales):
+            results = []
+            for first in range(0, DT, TILES_PER_BANK):
+                acc = psum.tile([P, TILES_PER_BANK, ROWS], F32, tag="bank")
+                for j in range(TILES_PER_BANK):
+                    cols = slice((first + j) * P, (first + j + 1) * P)
+                    nc.tensor.matmul_mx(
+                        out=acc[:, j, :],
+                        lhsT=w_codes[:, cols].bitcast(FP8X4),
+                        lhsT_scale=w_scales[:, cols],
+                        rhs=y_codes[:].bitcast(FP8X4),
+                        rhs_scale=y_scales[:],
+                        start=True,
+                        stop=True,
+                    )
+                    results.append(acc[:, j, :])
+            return results
+
+        sig_acc = project(wsig_codes, wsig_scales)
+        v = keep.tile([P, DT, ROWS], F32)
+        abs_v = keep.tile([P, DT, ROWS], F32)
+        exp_v = keep.tile([P, DT, ROWS], F32)
+        log_v = keep.tile([P, DT, ROWS], F32)
+        for dt in range(DT):
+            nc.vector.tensor_scalar(
+                out=v[:, dt, :], in0=sig_acc[dt],
+                scalar1=param(dt, ROW_BE_SIG), scalar2=None, op0=ALU.add,
+            )
+            nc.scalar.activation(out=abs_v[:, dt, :], in_=v[:, dt, :], func=ACT.Abs)
+        for dt in range(DT):
+            nc.scalar.activation(out=exp_v[:, dt, :], in_=abs_v[:, dt, :], func=ACT.Exp, scale=-1.0)
+        for dt in range(DT):
+            nc.scalar.activation(
+                out=log_v[:, dt, :], in_=exp_v[:, dt, :], func=ACT.Ln, bias=one_col[:]
+            )
+
+        wmu_codes = keep.tile([P, X_DIM], U32, align_bytes=64)
+        wmu_scales = keep.tile([P, X_DIM], U8, align_bytes=64)
+        quantise(wmu_codes, wmu_scales, wmu_grouped)
+        mu_acc = project(wmu_codes, wmu_scales)
+        muT = keep.tile([P, DT, ROWS], F32)
+        for dt in range(DT):
+            nc.vector.tensor_scalar(
+                out=muT[:, dt, :], in0=mu_acc[dt],
+                scalar1=param(dt, ROW_BE_MU), scalar2=None, op0=ALU.add,
+            )
+        relu_v = keep.tile([P, DT, ROWS], F32)
+        nc.vector.tensor_scalar_max(out=relu_v[:], in0=v[:], scalar1=0.0)
+
+        dist2 = keep.tile([P, CLUSTERS, DT, ROWS], F32)
+
+        def vector_difference(unit):
+            k, part = divmod(unit, UNITS_PER_CLUSTER)
+            diff = diffs.tile([P, UNIT_TILES, ROWS], F32)
+            for j in range(UNIT_TILES):
+                dt = part * UNIT_TILES + j
+                nc.vector.tensor_scalar(
+                    out=diff[:, j, :], in0=muT[:, dt, :],
+                    scalar1=param(dt, ROW_PHI_MU + k), scalar2=None, op0=ALU.subtract,
+                )
+            return diff
+
+        def square(engine, unit, diff):
+            k, part = divmod(unit, UNITS_PER_CLUSTER)
+            tiles = slice(part * UNIT_TILES, (part + 1) * UNIT_TILES)
+            engine.tensor_tensor(out=dist2[:, k, tiles, :], in0=diff[:], in1=diff[:], op=ALU.mult)
+
+        def gpsimd_square(unit):
+            k, part = divmod(unit, UNITS_PER_CLUSTER)
+            diff = diffs.tile([P, UNIT_TILES, ROWS], F32)
+            for j in range(UNIT_TILES):
+                dt = part * UNIT_TILES + j
+                nc.gpsimd.tensor_scalar(
+                    out=diff[:, j, :], in0=muT[:, dt, :],
+                    scalar1=-1.0, scalar2=param(dt, ROW_PHI_MU + k), op0=ALU.mult, op1=ALU.add,
+                )
+            square(nc.gpsimd, unit, diff)
+
+        def scalar_square(block):
+            k, dt = divmod(VECTOR_CLUSTERS * DT + block, DT)
+            nc.scalar.activation(
+                out=dist2[:, k, dt, :], in_=muT[:, dt, :], func=ACT.Square,
+                scale=-1.0, bias=param(dt, ROW_PHI_MU + k),
+            )
+
+        for block in range(SCALAR_LEAD):
+            scalar_square(block)
+
+        sigT = keep.tile([P, DT, ROWS], F32)
+        for dt in range(DT):
+            nc.vector.scalar_tensor_tensor(
+                out=sigT[:, dt, :], in0=log_v[:, dt, :], scalar=SIG_FLOOR, in1=relu_v[:, dt, :],
+                op0=ALU.add, op1=ALU.add,
+            )
+
+        def rows_onto_partitions(src):
+            bank = psum.tile([P, X_DIM], F32, tag="bank")
+            for dt in range(DT):
+                nc.tensor.transpose(bank[:, dt * P : (dt + 1) * P], src[:, dt, :], ident[:])
+            return bank
+
+        ln_std = keep.tile([P, CLUSTERS, NT, X_DIM], F32)
+        ln_sum = keep.tile([P, NT, CLUSTERS], F32)
+        for k in range(CLUSTERS):
+            if k >= VECTOR_START:
+                diff = vector_difference(k - VECTOR_START)
+            stdT = work.tile([P, DT, ROWS], F32)
+            for dt in range(DT):
+                nc.vector.tensor_scalar(
+                    out=stdT[:, dt, :], in0=sigT[:, dt, :],
+                    scalar1=param(dt, ROW_PHI_SIG + k), scalar2=None, op0=ALU.add,
+                )
+            for nt in range(NT):
+                std_bank = rows_onto_partitions(stdT[:, :, nt * P : (nt + 1) * P])
+                nc.scalar.activation(
+                    out=ln_std[:, k, nt, :], in_=std_bank[:], func=ACT.Ln,
+                    accum_out=ln_sum[:, nt, k : k + 1],
+                )
+            if k >= VECTOR_START:
+                square(nc.vector, k - VECTOR_START, diff)
+
+        rest = range(VECTOR_UNITS - VECTOR_REST, VECTOR_UNITS)
+        rest_diffs = [vector_difference(unit) for unit in rest]
+        for unit, diff in zip(rest, rest_diffs):
+            square(nc.vector, unit, diff)
+        for unit in range(GPSIMD_FIRST_UNIT, ALL_UNITS):
+            gpsimd_square(unit)
+
+        base = keep.tile([P, NT, CLUSTERS], F32)
+        nc.vector.tensor_tensor(
+            out=base[:], in0=logits[:].unsqueeze(1).to_broadcast([P, NT, CLUSTERS]), in1=ln_sum[:],
+            op=ALU.subtract,
+        )
+
+        maha_sum = keep.tile([P, NT, CLUSTERS], F32)
+        for k in range(CLUSTERS):
+            inv_var = work.tile([P, NT, X_DIM], F32)
+            nc.scalar.activation(out=inv_var[:], in_=ln_std[:, k, :, :], func=ACT.Exp, scale=-2.0)
+            if SCALAR_LEAD + k < SCALAR_BLOCKS:
+                scalar_square(SCALAR_LEAD + k)
+            for nt in range(NT):
+                dist2_bank = rows_onto_partitions(dist2[:, k, :, nt * P : (nt + 1) * P])
+                product = work.tile([P, X_DIM], F32)
+                nc.vector.scalar_tensor_tensor(
+                    out=product[:], in0=dist2_bank[:], scalar=0.5, in1=inv_var[:, nt, :],
+                    op0=ALU.mult, op1=ALU.mult, accum_out=maha_sum[:, nt, k : k + 1],
+                )
+
+        def store_rows(copy, dram, src):
+            for nt in range(NT):
+                bank = rows_onto_partitions(src[:, :, nt * P : (nt + 1) * P])
+                rows_sb = outs.tile([P, X_DIM], F32)
+                copy(out=rows_sb[:], in_=bank[:])
+                nc.sync.dma_start(out=dram[nt * P : (nt + 1) * P, :], in_=rows_sb[:])
+
+        store_rows(nc.scalar.copy, out_0, muT)
+
+        z = keep.tile([P, NT, CLUSTERS], F32)
+        nc.vector.tensor_tensor(out=z[:], in0=base[:], in1=maha_sum[:], op=ALU.subtract)
+        z_max = keep.tile([P, NT], F32)
+        nc.vector.tensor_reduce(out=z_max[:], in_=z[:], axis=AXIS.X, op=ALU.max)
+        z_shift = keep.tile([P, NT, CLUSTERS], F32)
+        nc.vector.tensor_tensor(
+            out=z_shift[:], in0=z[:], in1=z_max[:].unsqueeze(2).to_broadcast([P, NT, CLUSTERS]),
+            op=ALU.subtract,
+        )
+        exp_z = keep.tile([P, NT, CLUSTERS], F32)
+        exp_sum = keep.tile([P, NT], F32)
+        for nt in range(NT):
+            nc.scalar.activation(
+                out=exp_z[:, nt, :], in_=z_shift[:, nt, :], func=ACT.Exp,
+                accum_out=exp_sum[:, nt : nt + 1],
+            )
+        log_sum = keep.tile([P, NT], F32)
+        nc.scalar.activation(out=log_sum[:], in_=exp_sum[:], func=ACT.Ln)
+
+        store_rows(nc.vector.tensor_copy, out_1, sigT)
+
+        z_log_probs = keep.tile([P, NT, CLUSTERS], F32)
+        nc.vector.tensor_tensor(
+            out=z_log_probs[:], in0=z_shift[:],
+            in1=log_sum[:].unsqueeze(2).to_broadcast([P, NT, CLUSTERS]), op=ALU.subtract,
+        )
+        nc.sync.dma_start(out=out_2.rearrange("(t p) k -> p t k", p=P), in_=z_log_probs[:])

@@ -14,13 +14,14 @@ AXIS = mybir.AxisListType
 
 P = 128
 PSUM_BANKS = 8
-BANK_F32 = 512
 
 ROWS = 256
 Y_DIM = 512
 X_DIM = 512
 CLUSTERS = 16
 SIG_FLOOR = 1e-3
+EXP_CAP = 30.0
+QUADRANT = 32
 NT = ROWS // P
 DT = X_DIM // P
 
@@ -28,8 +29,8 @@ PACK = 4
 PAIR = 2
 WORDS = PACK // PAIR
 assert Y_DIM == P * PACK
+TILES_PER_BANK = 2
 RUN = 4
-TILES_PER_BANK = BANK_F32 // ROWS
 
 ROW_PHI_MU = 0
 ROW_PHI_SIG = CLUSTERS
@@ -37,17 +38,16 @@ ROW_BE_MU = 2 * CLUSTERS
 ROW_BE_SIG = 2 * CLUSTERS + 1
 PARAM_ROWS = 2 * CLUSTERS + 2
 
-VECTOR_CLUSTERS = 8
-SCALAR_CLUSTERS = 4
+VECTOR_CLUSTERS = 11
+SCALAR_CLUSTERS = 1
 UNIT_TILES = DT // 2
 UNITS_PER_CLUSTER = DT // UNIT_TILES
 VECTOR_UNITS = VECTOR_CLUSTERS * UNITS_PER_CLUSTER
 GPSIMD_FIRST_UNIT = (VECTOR_CLUSTERS + SCALAR_CLUSTERS) * UNITS_PER_CLUSTER
 ALL_UNITS = CLUSTERS * UNITS_PER_CLUSTER
-VECTOR_START = PSUM_BANKS // NT
-VECTOR_REST = VECTOR_UNITS - (CLUSTERS - VECTOR_START)
-SCALAR_BLOCKS = SCALAR_CLUSTERS * DT
-SCALAR_LEAD = SCALAR_BLOCKS // 2
+VECTOR_REST = 4
+VECTOR_LOOP_UNITS = VECTOR_UNITS - VECTOR_REST
+VECTOR_ADDS_EVERY = 4
 
 FLOPS = 2 * 2 * ROWS * Y_DIM * X_DIM
 
@@ -64,17 +64,19 @@ def tile_deepgmm_pa_s_kernel(
         def load_weight(raw, w):
             nc.sync.dma_start(out=raw[:], in_=w.rearrange("(p t) c -> p t c", t=PACK))
 
-        def group(grouped, raw):
-            nc.vector.tensor_copy(
-                out=grouped[:].rearrange("p (c i) t -> p c t i", i=RUN),
-                in_=raw[:].rearrange("p t (c i) -> p c t i", i=RUN),
+        def group(copy, grouped, raw, dt):
+            cols = slice(dt * P, (dt + 1) * P)
+            copy(
+                out=grouped[:, cols, :].rearrange("p (c i) t -> p c t i", i=RUN),
+                in_=raw[:, :, cols].rearrange("p t (c i) -> p c t i", i=RUN),
             )
 
-        def quantise(codes, scales, grouped):
+        def quantise(codes, scales, grouped, tile):
+            cols = slice(tile * P, (tile + 1) * P)
             nc.vector.quantize_mx(
-                out=codes[:].bitcast(FP8X4),
-                scales=scales[:],
-                in_=grouped[:].rearrange("p c t -> p (c t)"),
+                out=codes[:, cols].bitcast(FP8X4),
+                scales=scales[:, cols],
+                in_=grouped[:, cols, :].rearrange("p c t -> p (c t)"),
             )
 
         ident = keep.tile([P, P], F32)
@@ -86,123 +88,137 @@ def tile_deepgmm_pa_s_kernel(
         y_scales = keep.tile([P, ROWS], U8, align_bytes=64)
         wsig_codes = keep.tile([P, X_DIM], U32, align_bytes=64)
         wsig_scales = keep.tile([P, X_DIM], U8, align_bytes=64)
-        wmu_raw = keep.tile([P, PACK, X_DIM], BF16)
+        wmu_codes = keep.tile([P, X_DIM], U32, align_bytes=64)
+        wmu_scales = keep.tile([P, X_DIM], U8, align_bytes=64)
         logits = keep.tile([P, CLUSTERS], BF16)
         params = keep.tile([P, DT, PARAM_ROWS], F32)
-
-        with tc.tile_pool(name="early", bufs=1) as early:
-            param_rows = early.tile([P, X_DIM], BF16)
-            nc.vector.memset(param_rows[:], 0.0)
-
-            y_sb = early.tile([P, NT, Y_DIM], BF16)
-            nc.sync.dma_start(out=y_sb[:], in_=Y.rearrange("(t p) k -> p t k", p=P))
-            wsig_raw = early.tile([P, PACK, X_DIM], BF16)
-            load_weight(wsig_raw, We_sig)
-            load_weight(wmu_raw, We_mu)
-            nc.sync.dma_start(out=logits[:], in_=phi_logits.partition_broadcast(P))
-
-            nc.scalar.dma_start(
-                out=param_rows[ROW_PHI_SIG : ROW_PHI_SIG + CLUSTERS, :], in_=phi_sigs
-            )
-            nc.scalar.dma_start(out=param_rows[ROW_PHI_MU : ROW_PHI_MU + CLUSTERS, :], in_=phi_mus)
-            nc.scalar.dma_start(
-                out=param_rows[ROW_BE_SIG : ROW_BE_SIG + 1, :],
-                in_=be_sig.rearrange("(o d) -> o d", o=1),
-            )
-            nc.scalar.dma_start(
-                out=param_rows[ROW_BE_MU : ROW_BE_MU + 1, :],
-                in_=be_mu.rearrange("(o d) -> o d", o=1),
-            )
-
-            warm = keep.tile([P, 1], F32)
-            nc.scalar.activation(out=warm[:], in_=one_col[:], func=ACT.Exp)
-
-            y_words = y_sb[:].bitcast(F32)
-            yT_ps = psum.tile([P, WORDS, ROWS], F32, tag="bank")
-            for nt in range(NT):
-                for u in range(WORDS):
-                    nc.tensor.transpose(
-                        yT_ps[:, u, nt * P : (nt + 1) * P],
-                        y_words[:, nt, u : WORDS * P : WORDS],
-                        ident[:],
-                    )
-            y_grouped = early.tile([P, ROWS, PACK], BF16, align_bytes=64)
-            nc.vector.tensor_copy(
-                out=y_grouped[:].bitcast(F32), in_=yT_ps[:].rearrange("p u n -> p n u")
-            )
-
-            param_rows_f = early.tile([P, X_DIM], F32)
-            nc.scalar.copy(out=param_rows_f[:], in_=param_rows[:])
-            param_ps = psum.tile([P, DT, P], F32, tag="bank")
-            for dt in range(DT):
-                nc.tensor.transpose(
-                    param_ps[:, dt, :], param_rows_f[:, dt * P : (dt + 1) * P], ident[:]
-                )
-            nc.scalar.copy(out=params[:], in_=param_ps[:, :, 0:PARAM_ROWS])
-
-            wsig_grouped = early.tile([P, X_DIM, PACK], BF16, align_bytes=64)
-            group(wsig_grouped, wsig_raw)
-            quantise(y_codes, y_scales, y_grouped)
-            quantise(wsig_codes, wsig_scales, wsig_grouped)
-
-        work = ctx.enter_context(tc.tile_pool(name="work", bufs=3))
-        outs = ctx.enter_context(tc.tile_pool(name="outs", bufs=2 * NT))
-        diffs = ctx.enter_context(tc.tile_pool(name="diffs", bufs=VECTOR_REST))
+        floor_sig = keep.tile([P, DT, CLUSTERS], F32)
+        muT = keep.tile([P, DT, ROWS], F32)
+        sigT = keep.tile([P, DT, ROWS], F32)
 
         def param(dt, row):
             return params[:, dt, row : row + 1]
 
-        wmu_grouped = keep.tile([P, X_DIM, PACK], BF16, align_bytes=64)
-        group(wmu_grouped, wmu_raw)
+        def project(out, w_codes, w_scales, dt):
+            cols = slice(dt * P, (dt + 1) * P)
+            nc.tensor.matmul_mx(
+                out=out,
+                lhsT=w_codes[:, cols].bitcast(FP8X4),
+                lhsT_scale=w_scales[:, cols],
+                rhs=y_codes[:].bitcast(FP8X4),
+                rhs_scale=y_scales[:],
+                start=True,
+                stop=True,
+            )
 
-        def project(w_codes, w_scales):
-            results = []
-            for first in range(0, DT, TILES_PER_BANK):
-                acc = psum.tile([P, TILES_PER_BANK, ROWS], F32, tag="bank")
-                for j in range(TILES_PER_BANK):
-                    cols = slice((first + j) * P, (first + j + 1) * P)
-                    nc.tensor.matmul_mx(
-                        out=acc[:, j, :],
-                        lhsT=w_codes[:, cols].bitcast(FP8X4),
-                        lhsT_scale=w_scales[:, cols],
-                        rhs=y_codes[:].bitcast(FP8X4),
-                        rhs_scale=y_scales[:],
-                        start=True,
-                        stop=True,
+        with tc.tile_pool(name="early", bufs=1) as early:
+            param_rows = early.tile([P, X_DIM], BF16)
+            nc.vector.memset(param_rows[QUADRANT : 2 * QUADRANT, :], 0.0)
+            nc.vector.memset(param_rows[2 * QUADRANT :, :], 0.0)
+
+            y_sb = early.tile([P, NT, Y_DIM], BF16)
+            nc.sync.dma_start(out=y_sb[:], in_=Y.rearrange("(t p) k -> p t k", p=P))
+            for row, rows in (
+                (ROW_PHI_SIG, phi_sigs),
+                (ROW_PHI_MU, phi_mus),
+                (ROW_BE_SIG, be_sig.rearrange("(o d) -> o d", o=1)),
+                (ROW_BE_MU, be_mu.rearrange("(o d) -> o d", o=1)),
+            ):
+                nc.sync.dma_start(out=param_rows[row : row + rows.shape[0], :], in_=rows)
+            wsig_raw = early.tile([P, PACK, X_DIM], BF16)
+            wmu_raw = early.tile([P, PACK, X_DIM], BF16)
+            load_weight(wsig_raw, We_sig)
+            load_weight(wmu_raw, We_mu)
+            nc.sync.dma_start(out=logits[:], in_=phi_logits.partition_broadcast(P))
+
+            warm = keep.tile([P, 1], F32)
+            nc.scalar.activation(out=warm[:], in_=one_col[:], func=ACT.Exp)
+
+            ident_bf = early.tile([P, P], BF16)
+            nc.vector.tensor_copy(out=ident_bf[:], in_=ident[:])
+
+            y_words = y_sb[:].bitcast(F32)
+            y_banks = []
+            for nt in range(NT):
+                yT_ps = psum.tile([P, WORDS, P], F32, tag="bank")
+                for u in range(WORDS):
+                    nc.tensor.transpose(
+                        yT_ps[:, u, :], y_words[:, nt, u : WORDS * P : WORDS], ident[:]
                     )
-                    results.append(acc[:, j, :])
-            return results
+                y_banks.append(yT_ps)
 
-        sig_acc = project(wsig_codes, wsig_scales)
-        v = keep.tile([P, DT, ROWS], F32)
-        abs_v = keep.tile([P, DT, ROWS], F32)
-        exp_v = keep.tile([P, DT, ROWS], F32)
-        log_v = keep.tile([P, DT, ROWS], F32)
-        for dt in range(DT):
-            nc.vector.tensor_scalar(
-                out=v[:, dt, :], in0=sig_acc[dt],
-                scalar1=param(dt, ROW_BE_SIG), scalar2=None, op0=ALU.add,
-            )
-            nc.scalar.activation(out=abs_v[:, dt, :], in_=v[:, dt, :], func=ACT.Abs)
-        for dt in range(DT):
-            nc.scalar.activation(out=exp_v[:, dt, :], in_=abs_v[:, dt, :], func=ACT.Exp, scale=-1.0)
-        for dt in range(DT):
-            nc.scalar.activation(
-                out=log_v[:, dt, :], in_=exp_v[:, dt, :], func=ACT.Ln, bias=one_col[:]
-            )
+            param_ps = psum.tile([P, DT, P], BF16, tag="bank")
+            for dt in range(DT):
+                nc.tensor.transpose(
+                    param_ps[:, dt, :], param_rows[:, dt * P : (dt + 1) * P], ident_bf[:]
+                )
+            nc.scalar.copy(out=params[:], in_=param_ps[:, :, 0:PARAM_ROWS])
 
-        wmu_codes = keep.tile([P, X_DIM], U32, align_bytes=64)
-        wmu_scales = keep.tile([P, X_DIM], U8, align_bytes=64)
-        quantise(wmu_codes, wmu_scales, wmu_grouped)
-        mu_acc = project(wmu_codes, wmu_scales)
-        muT = keep.tile([P, DT, ROWS], F32)
-        for dt in range(DT):
+            y_grouped = early.tile([P, ROWS, PACK], BF16, align_bytes=64)
+            for nt in range(NT):
+                nc.vector.tensor_copy(
+                    out=y_grouped[:].bitcast(F32)[:, nt * P : (nt + 1) * P, :],
+                    in_=y_banks[nt][:].rearrange("p u n -> p n u"),
+                )
+            for nt in range(NT):
+                quantise(y_codes, y_scales, y_grouped, nt)
+
+            wsig_grouped = early.tile([P, X_DIM, PACK], BF16, align_bytes=64)
+            group(nc.scalar.copy, wsig_grouped, wsig_raw, DT - 1)
+            group(nc.vector.tensor_copy, wsig_grouped, wsig_raw, 0)
+            for dt in range(DT):
+                if dt + 1 < DT - 1:
+                    group(nc.vector.tensor_copy, wsig_grouped, wsig_raw, dt + 1)
+                quantise(wsig_codes, wsig_scales, wsig_grouped, dt)
+            sig_acc = []
+            for dt in range(DT):
+                acc = psum.tile([P, ROWS], F32, tag="bank")
+                project(acc[:], wsig_codes, wsig_scales, dt)
+                sig_acc.append(acc)
+
+            cap_v = early.tile([P, DT, ROWS], F32)
+            exp_v = early.tile([P, DT, ROWS], F32)
+            log_v = early.tile([P, DT, ROWS], F32)
+            for dt in range(DT):
+                nc.vector.tensor_scalar(
+                    out=cap_v[:, dt, :], in0=sig_acc[dt][:],
+                    scalar1=param(dt, ROW_BE_SIG), scalar2=EXP_CAP, op0=ALU.add, op1=ALU.min,
+                )
+                nc.scalar.activation(out=exp_v[:, dt, :], in_=cap_v[:, dt, :], func=ACT.Exp)
+            for dt in range(DT):
+                nc.scalar.activation(
+                    out=log_v[:, dt, :], in_=exp_v[:, dt, :], func=ACT.Ln, bias=one_col[:]
+                )
+
+            wmu_grouped = early.tile([P, X_DIM, PACK], BF16, align_bytes=64)
+            group(nc.vector.tensor_copy, wmu_grouped, wmu_raw, 0)
+            for dt in range(DT):
+                if dt + 1 < DT:
+                    group(nc.vector.tensor_copy, wmu_grouped, wmu_raw, dt + 1)
+                quantise(wmu_codes, wmu_scales, wmu_grouped, dt)
             nc.vector.tensor_scalar(
-                out=muT[:, dt, :], in0=mu_acc[dt],
-                scalar1=param(dt, ROW_BE_MU), scalar2=None, op0=ALU.add,
+                out=floor_sig[:], in0=params[:, :, ROW_PHI_SIG : ROW_PHI_SIG + CLUSTERS],
+                scalar1=SIG_FLOOR, scalar2=None, op0=ALU.add,
             )
-        relu_v = keep.tile([P, DT, ROWS], F32)
-        nc.vector.tensor_scalar_max(out=relu_v[:], in0=v[:], scalar1=0.0)
+            for first in range(0, DT, TILES_PER_BANK):
+                mu_acc = psum.tile([P, TILES_PER_BANK, ROWS], F32, tag="bank")
+                for j in range(TILES_PER_BANK):
+                    project(mu_acc[:, j, :], wmu_codes, wmu_scales, first + j)
+                for j in range(TILES_PER_BANK):
+                    nc.vector.tensor_scalar(
+                        out=muT[:, first + j, :], in0=mu_acc[:, j, :],
+                        scalar1=param(first + j, ROW_BE_MU), scalar2=None, op0=ALU.add,
+                    )
+
+            for dt in range(DT):
+                nc.vector.scalar_tensor_tensor(
+                    out=sigT[:, dt, :], in0=sig_acc[dt][:], scalar=param(dt, ROW_BE_SIG),
+                    in1=log_v[:, dt, :], op0=ALU.add, op1=ALU.max,
+                )
+
+        work = ctx.enter_context(tc.tile_pool(name="work", bufs=3))
+        outs = ctx.enter_context(tc.tile_pool(name="outs", bufs=2 * NT))
+        diffs = ctx.enter_context(tc.tile_pool(name="diffs", bufs=VECTOR_REST))
 
         dist2 = keep.tile([P, CLUSTERS, DT, ROWS], F32)
 
@@ -240,15 +256,8 @@ def tile_deepgmm_pa_s_kernel(
                 scale=-1.0, bias=param(dt, ROW_PHI_MU + k),
             )
 
-        for block in range(SCALAR_LEAD):
+        for block in range(SCALAR_CLUSTERS * DT):
             scalar_square(block)
-
-        sigT = keep.tile([P, DT, ROWS], F32)
-        for dt in range(DT):
-            nc.vector.scalar_tensor_tensor(
-                out=sigT[:, dt, :], in0=log_v[:, dt, :], scalar=SIG_FLOOR, in1=relu_v[:, dt, :],
-                op0=ALU.add, op1=ALU.add,
-            )
 
         def rows_onto_partitions(src):
             bank = psum.tile([P, X_DIM], F32, tag="bank")
@@ -256,30 +265,54 @@ def tile_deepgmm_pa_s_kernel(
                 nc.tensor.transpose(bank[:, dt * P : (dt + 1) * P], src[:, dt, :], ident[:])
             return bank
 
+        def std_rows(k, nt):
+            bank = psum.tile([P, X_DIM], F32, tag="bank")
+            for dt in range(DT):
+                for src, first in (
+                    (sigT[:, dt, nt * P : (nt + 1) * P], True),
+                    (floor_sig[:, dt, k : k + 1].to_broadcast([P, P]), False),
+                ):
+                    nc.tensor.matmul(
+                        bank[:, dt * P : (dt + 1) * P], lhsT=src, rhs=ident[:],
+                        start=first, stop=not first, is_transpose=True,
+                    )
+            return bank
+
         ln_std = keep.tile([P, CLUSTERS, NT, X_DIM], F32)
         ln_sum = keep.tile([P, NT, CLUSTERS], F32)
+        not_squared = []
+
+        def vector_units(units):
+            for unit in units:
+                diff = vector_difference(unit)
+                if not_squared:
+                    square(nc.vector, *not_squared.pop())
+                not_squared.append((unit, diff))
+
         for k in range(CLUSTERS):
-            if k >= VECTOR_START:
-                diff = vector_difference(k - VECTOR_START)
-            stdT = work.tile([P, DT, ROWS], F32)
-            for dt in range(DT):
-                nc.vector.tensor_scalar(
-                    out=stdT[:, dt, :], in0=sigT[:, dt, :],
-                    scalar1=param(dt, ROW_PHI_SIG + k), scalar2=None, op0=ALU.add,
-                )
+            vector_adds = k % VECTOR_ADDS_EVERY == VECTOR_ADDS_EVERY - 1
+            if vector_adds:
+                stdT = work.tile([P, DT, ROWS], F32)
+                for dt in range(DT):
+                    nc.vector.tensor_scalar(
+                        out=stdT[:, dt, :], in0=sigT[:, dt, :],
+                        scalar1=floor_sig[:, dt, k : k + 1], scalar2=None, op0=ALU.add,
+                    )
             for nt in range(NT):
-                std_bank = rows_onto_partitions(stdT[:, :, nt * P : (nt + 1) * P])
+                if vector_adds:
+                    std_bank = rows_onto_partitions(stdT[:, :, nt * P : (nt + 1) * P])
+                else:
+                    std_bank = std_rows(k, nt)
                 nc.scalar.activation(
                     out=ln_std[:, k, nt, :], in_=std_bank[:], func=ACT.Ln,
                     accum_out=ln_sum[:, nt, k : k + 1],
                 )
-            if k >= VECTOR_START:
-                square(nc.vector, k - VECTOR_START, diff)
+            vector_units(
+                range(k * VECTOR_LOOP_UNITS // CLUSTERS, (k + 1) * VECTOR_LOOP_UNITS // CLUSTERS)
+            )
 
-        rest = range(VECTOR_UNITS - VECTOR_REST, VECTOR_UNITS)
-        rest_diffs = [vector_difference(unit) for unit in rest]
-        for unit, diff in zip(rest, rest_diffs):
-            square(nc.vector, unit, diff)
+        vector_units(range(VECTOR_LOOP_UNITS, VECTOR_UNITS))
+        square(nc.vector, *not_squared.pop())
         for unit in range(GPSIMD_FIRST_UNIT, ALL_UNITS):
             gpsimd_square(unit)
 
@@ -293,8 +326,6 @@ def tile_deepgmm_pa_s_kernel(
         for k in range(CLUSTERS):
             inv_var = work.tile([P, NT, X_DIM], F32)
             nc.scalar.activation(out=inv_var[:], in_=ln_std[:, k, :, :], func=ACT.Exp, scale=-2.0)
-            if SCALAR_LEAD + k < SCALAR_BLOCKS:
-                scalar_square(SCALAR_LEAD + k)
             for nt in range(NT):
                 dist2_bank = rows_onto_partitions(dist2[:, k, :, nt * P : (nt + 1) * P])
                 product = work.tile([P, X_DIM], F32)
@@ -307,10 +338,10 @@ def tile_deepgmm_pa_s_kernel(
             for nt in range(NT):
                 bank = rows_onto_partitions(src[:, :, nt * P : (nt + 1) * P])
                 rows_sb = outs.tile([P, X_DIM], F32)
-                copy(out=rows_sb[:], in_=bank[:])
+                copy(rows_sb[:], bank[:])
                 nc.sync.dma_start(out=dram[nt * P : (nt + 1) * P, :], in_=rows_sb[:])
 
-        store_rows(nc.scalar.copy, out_0, muT)
+        store_rows(lambda out, in_: nc.scalar.copy(out=out, in_=in_), out_0, muT)
 
         z = keep.tile([P, NT, CLUSTERS], F32)
         nc.vector.tensor_tensor(out=z[:], in0=base[:], in1=maha_sum[:], op=ALU.subtract)
@@ -331,7 +362,11 @@ def tile_deepgmm_pa_s_kernel(
         log_sum = keep.tile([P, NT], F32)
         nc.scalar.activation(out=log_sum[:], in_=exp_sum[:], func=ACT.Ln)
 
-        store_rows(nc.vector.tensor_copy, out_1, sigT)
+        store_rows(
+            lambda out, in_: nc.vector.tensor_scalar_add(out=out, in0=in_, scalar1=SIG_FLOOR),
+            out_1,
+            sigT,
+        )
 
         z_log_probs = keep.tile([P, NT, CLUSTERS], F32)
         nc.vector.tensor_tensor(

@@ -38,13 +38,15 @@ ROW_BE_MU = 2 * CLUSTERS
 ROW_BE_SIG = 2 * CLUSTERS + 1
 PARAM_ROWS = 2 * CLUSTERS + 2
 
-VECTOR_CLUSTERS = 11
-SCALAR_CLUSTERS = 1
+VECTOR_CLUSTERS = 9
+SCALAR_CLUSTERS = 3
 UNIT_TILES = DT // 2
 UNITS_PER_CLUSTER = DT // UNIT_TILES
 VECTOR_UNITS = VECTOR_CLUSTERS * UNITS_PER_CLUSTER
 GPSIMD_FIRST_UNIT = (VECTOR_CLUSTERS + SCALAR_CLUSTERS) * UNITS_PER_CLUSTER
 ALL_UNITS = CLUSTERS * UNITS_PER_CLUSTER
+SCALAR_BLOCKS = SCALAR_CLUSTERS * DT
+SCALAR_LEAD = DT
 VECTOR_REST = 4
 VECTOR_LOOP_UNITS = VECTOR_UNITS - VECTOR_REST
 VECTOR_ADDS_EVERY = 4
@@ -256,7 +258,7 @@ def tile_deepgmm_pa_s_kernel(
                 scale=-1.0, bias=param(dt, ROW_PHI_MU + k),
             )
 
-        for block in range(SCALAR_CLUSTERS * DT):
+        for block in range(SCALAR_LEAD):
             scalar_square(block)
 
         def rows_onto_partitions(src):
@@ -325,7 +327,12 @@ def tile_deepgmm_pa_s_kernel(
         maha_sum = keep.tile([P, NT, CLUSTERS], F32)
         for k in range(CLUSTERS):
             inv_var = work.tile([P, NT, X_DIM], F32)
-            nc.scalar.activation(out=inv_var[:], in_=ln_std[:, k, :, :], func=ACT.Exp, scale=-2.0)
+            for rows in [slice(nt, nt + 1) for nt in range(NT)] if k == 0 else [slice(0, NT)]:
+                nc.scalar.activation(
+                    out=inv_var[:, rows, :], in_=ln_std[:, k, rows, :], func=ACT.Exp, scale=-2.0
+                )
+            if SCALAR_LEAD + k < SCALAR_BLOCKS:
+                scalar_square(SCALAR_LEAD + k)
             for nt in range(NT):
                 dist2_bank = rows_onto_partitions(dist2[:, k, :, nt * P : (nt + 1) * P])
                 product = work.tile([P, X_DIM], F32)

@@ -49,7 +49,7 @@ SCALAR_BLOCKS = SCALAR_CLUSTERS * DT
 SCALAR_LEAD = DT
 VECTOR_REST = 4
 VECTOR_LOOP_UNITS = VECTOR_UNITS - VECTOR_REST
-VECTOR_ADDS_EVERY = 4
+VECTOR_ADDS_EVERY = 2
 
 FLOPS = 2 * 2 * ROWS * Y_DIM * X_DIM
 

@@ -38,18 +38,24 @@ ROW_BE_MU = 2 * CLUSTERS
 ROW_BE_SIG = 2 * CLUSTERS + 1
 PARAM_ROWS = 2 * CLUSTERS + 2
 
-VECTOR_CLUSTERS = 9
-SCALAR_CLUSTERS = 3
+VECTOR_CLUSTERS = 10
+SCALAR_CLUSTERS = 2
 UNIT_TILES = DT // 2
 UNITS_PER_CLUSTER = DT // UNIT_TILES
 VECTOR_UNITS = VECTOR_CLUSTERS * UNITS_PER_CLUSTER
 GPSIMD_FIRST_UNIT = (VECTOR_CLUSTERS + SCALAR_CLUSTERS) * UNITS_PER_CLUSTER
 ALL_UNITS = CLUSTERS * UNITS_PER_CLUSTER
 SCALAR_BLOCKS = SCALAR_CLUSTERS * DT
-SCALAR_LEAD = DT
 VECTOR_REST = 4
 VECTOR_LOOP_UNITS = VECTOR_UNITS - VECTOR_REST
-VECTOR_ADDS_EVERY = 2
+
+
+def d_on_partitions(k):
+    return k % 2 == 0
+
+
+FOLD_LAG = 3
+SUM_LAG = 5
 
 FLOPS = 2 * 2 * ROWS * Y_DIM * X_DIM
 
@@ -221,6 +227,7 @@ def tile_deepgmm_pa_s_kernel(
         work = ctx.enter_context(tc.tile_pool(name="work", bufs=3))
         outs = ctx.enter_context(tc.tile_pool(name="outs", bufs=2 * NT))
         diffs = ctx.enter_context(tc.tile_pool(name="diffs", bufs=VECTOR_REST))
+        ln_pool = ctx.enter_context(tc.tile_pool(name="ln_pool", bufs=CLUSTERS))
 
         dist2 = keep.tile([P, CLUSTERS, DT, ROWS], F32)
 
@@ -258,9 +265,6 @@ def tile_deepgmm_pa_s_kernel(
                 scale=-1.0, bias=param(dt, ROW_PHI_MU + k),
             )
 
-        for block in range(SCALAR_LEAD):
-            scalar_square(block)
-
         def rows_onto_partitions(src):
             bank = psum.tile([P, X_DIM], F32, tag="bank")
             for dt in range(DT):
@@ -280,7 +284,8 @@ def tile_deepgmm_pa_s_kernel(
                     )
             return bank
 
-        ln_std = keep.tile([P, CLUSTERS, NT, X_DIM], F32)
+        ln_rows = {}
+        ln_cols = {}
         ln_sum = keep.tile([P, NT, CLUSTERS], F32)
         not_squared = []
 
@@ -291,30 +296,57 @@ def tile_deepgmm_pa_s_kernel(
                     square(nc.vector, *not_squared.pop())
                 not_squared.append((unit, diff))
 
-        for k in range(CLUSTERS):
-            vector_adds = k % VECTOR_ADDS_EVERY == VECTOR_ADDS_EVERY - 1
-            if vector_adds:
-                stdT = work.tile([P, DT, ROWS], F32)
-                for dt in range(DT):
-                    nc.vector.tensor_scalar(
-                        out=stdT[:, dt, :], in0=sigT[:, dt, :],
-                        scalar1=floor_sig[:, dt, k : k + 1], scalar2=None, op0=ALU.add,
-                    )
+        folded = {}
+
+        def fold_d_tiles(k):
+            bank = psum.tile([P, NT, P], F32, tag="bank")
             for nt in range(NT):
-                if vector_adds:
-                    std_bank = rows_onto_partitions(stdT[:, :, nt * P : (nt + 1) * P])
-                else:
+                for dt in range(DT):
+                    nc.tensor.matmul(
+                        bank[:, nt, :], lhsT=ln_cols[k][:, dt, nt * P : (nt + 1) * P], rhs=ident[:],
+                        start=dt == 0, stop=dt == DT - 1, is_transpose=True,
+                    )
+            folded[k] = bank
+
+        def sum_folded(k):
+            nc.vector.tensor_reduce(
+                out=ln_sum[:, :, k], in_=folded[k][:], axis=AXIS.X, op=ALU.add
+            )
+
+        for k in range(CLUSTERS):
+            if d_on_partitions(k):
+                ln_std = ln_pool.tile([P, DT, ROWS], F32)
+                for dt in range(DT):
+                    nc.scalar.activation(
+                        out=ln_std[:, dt, :], in_=sigT[:, dt, :], func=ACT.Ln,
+                        bias=floor_sig[:, dt, k : k + 1],
+                    )
+                ln_cols[k] = ln_std
+            else:
+                ln_std = ln_pool.tile([P, NT, X_DIM], F32)
+                for nt in range(NT):
                     std_bank = std_rows(k, nt)
-                nc.scalar.activation(
-                    out=ln_std[:, k, nt, :], in_=std_bank[:], func=ACT.Ln,
-                    accum_out=ln_sum[:, nt, k : k + 1],
-                )
+                    nc.scalar.activation(
+                        out=ln_std[:, nt, :], in_=std_bank[:], func=ACT.Ln,
+                        accum_out=ln_sum[:, nt, k : k + 1],
+                    )
+                ln_rows[k] = ln_std
+            if k - FOLD_LAG in ln_cols:
+                fold_d_tiles(k - FOLD_LAG)
             vector_units(
                 range(k * VECTOR_LOOP_UNITS // CLUSTERS, (k + 1) * VECTOR_LOOP_UNITS // CLUSTERS)
             )
+            if k - SUM_LAG in folded:
+                sum_folded(k - SUM_LAG)
 
+        for k in range(CLUSTERS - FOLD_LAG, CLUSTERS):
+            if k in ln_cols:
+                fold_d_tiles(k)
         vector_units(range(VECTOR_LOOP_UNITS, VECTOR_UNITS))
         square(nc.vector, *not_squared.pop())
+        for k in range(CLUSTERS - SUM_LAG, CLUSTERS):
+            if k in folded:
+                sum_folded(k)
         for unit in range(GPSIMD_FIRST_UNIT, ALL_UNITS):
             gpsimd_square(unit)
 
@@ -325,14 +357,27 @@ def tile_deepgmm_pa_s_kernel(
         )
 
         maha_sum = keep.tile([P, NT, CLUSTERS], F32)
+
+        def ln_of_rows(k):
+            if k in ln_rows:
+                return [(slice(0, NT), ln_rows[k][:])]
+            pieces = []
+            for nt in range(NT):
+                bank = rows_onto_partitions(ln_cols[k][:, :, nt * P : (nt + 1) * P])
+                pieces.append((nt, bank[:]))
+            return pieces
+
+        pieces = ln_of_rows(0)
         for k in range(CLUSTERS):
             inv_var = work.tile([P, NT, X_DIM], F32)
-            for rows in [slice(nt, nt + 1) for nt in range(NT)] if k == 0 else [slice(0, NT)]:
+            for rows, ln_std in pieces:
                 nc.scalar.activation(
-                    out=inv_var[:, rows, :], in_=ln_std[:, k, rows, :], func=ACT.Exp, scale=-2.0
+                    out=inv_var[:, rows, :], in_=ln_std, func=ACT.Exp, scale=-2.0
                 )
-            if SCALAR_LEAD + k < SCALAR_BLOCKS:
-                scalar_square(SCALAR_LEAD + k)
+            if k < SCALAR_BLOCKS:
+                scalar_square(k)
+            if k + 1 < CLUSTERS:
+                pieces = ln_of_rows(k + 1)
             for nt in range(NT):
                 dist2_bank = rows_onto_partitions(dist2[:, k, :, nt * P : (nt + 1) * P])
                 product = work.tile([P, X_DIM], F32)
@@ -350,34 +395,32 @@ def tile_deepgmm_pa_s_kernel(
 
         store_rows(lambda out, in_: nc.scalar.copy(out=out, in_=in_), out_0, muT)
 
-        z = keep.tile([P, NT, CLUSTERS], F32)
-        nc.vector.tensor_tensor(out=z[:], in0=base[:], in1=maha_sum[:], op=ALU.subtract)
-        z_max = keep.tile([P, NT], F32)
-        nc.vector.tensor_reduce(out=z_max[:], in_=z[:], axis=AXIS.X, op=ALU.max)
-        z_shift = keep.tile([P, NT, CLUSTERS], F32)
-        nc.vector.tensor_tensor(
-            out=z_shift[:], in0=z[:], in1=z_max[:].unsqueeze(2).to_broadcast([P, NT, CLUSTERS]),
-            op=ALU.subtract,
-        )
+        neg_z = keep.tile([P, NT, CLUSTERS], F32)
+        nc.vector.tensor_tensor(out=neg_z[:], in0=maha_sum[:], in1=base[:], op=ALU.subtract)
+        low = keep.tile([P, NT], F32)
+        nc.vector.tensor_reduce(out=low[:], in_=neg_z[:], axis=AXIS.X, op=ALU.min)
         exp_z = keep.tile([P, NT, CLUSTERS], F32)
         exp_sum = keep.tile([P, NT], F32)
         for nt in range(NT):
             nc.scalar.activation(
-                out=exp_z[:, nt, :], in_=z_shift[:, nt, :], func=ACT.Exp,
-                accum_out=exp_sum[:, nt : nt + 1],
+                out=exp_z[:, nt, :], in_=neg_z[:, nt, :], func=ACT.Exp,
+                scale=-1.0, bias=low[:, nt : nt + 1], accum_out=exp_sum[:, nt : nt + 1],
             )
         log_sum = keep.tile([P, NT], F32)
         nc.scalar.activation(out=log_sum[:], in_=exp_sum[:], func=ACT.Ln)
-
+        shifted = keep.tile([P, NT, CLUSTERS], F32)
+        nc.vector.tensor_tensor(
+            out=shifted[:], in0=low[:].unsqueeze(2).to_broadcast([P, NT, CLUSTERS]), in1=neg_z[:],
+            op=ALU.subtract,
+        )
         store_rows(
             lambda out, in_: nc.vector.tensor_scalar_add(out=out, in0=in_, scalar1=SIG_FLOOR),
             out_1,
             sigT,
         )
-
         z_log_probs = keep.tile([P, NT, CLUSTERS], F32)
         nc.vector.tensor_tensor(
-            out=z_log_probs[:], in0=z_shift[:],
+            out=z_log_probs[:], in0=shifted[:],
             in1=log_sum[:].unsqueeze(2).to_broadcast([P, NT, CLUSTERS]), op=ALU.subtract,
         )
         nc.sync.dma_start(out=out_2.rearrange("(t p) k -> p t k", p=P), in_=z_log_probs[:])

@@ -38,14 +38,13 @@ ROW_BE_MU = 2 * CLUSTERS
 ROW_BE_SIG = 2 * CLUSTERS + 1
 PARAM_ROWS = 2 * CLUSTERS + 2
 
-VECTOR_CLUSTERS = 10
-SCALAR_CLUSTERS = 2
+VECTOR_UNITS = 21
+SCALAR_UNITS = 3
 UNIT_TILES = DT // 2
 UNITS_PER_CLUSTER = DT // UNIT_TILES
-VECTOR_UNITS = VECTOR_CLUSTERS * UNITS_PER_CLUSTER
-GPSIMD_FIRST_UNIT = (VECTOR_CLUSTERS + SCALAR_CLUSTERS) * UNITS_PER_CLUSTER
+GPSIMD_FIRST_UNIT = VECTOR_UNITS + SCALAR_UNITS
 ALL_UNITS = CLUSTERS * UNITS_PER_CLUSTER
-SCALAR_BLOCKS = SCALAR_CLUSTERS * DT
+SCALAR_BLOCKS = SCALAR_UNITS * UNIT_TILES
 VECTOR_REST = 4
 VECTOR_LOOP_UNITS = VECTOR_UNITS - VECTOR_REST
 
@@ -72,25 +71,28 @@ def tile_deepgmm_pa_s_kernel(
         def load_weight(raw, w):
             nc.sync.dma_start(out=raw[:], in_=w.rearrange("(p t) c -> p t c", t=PACK))
 
-        def group(copy, grouped, raw, dt):
-            cols = slice(dt * P, (dt + 1) * P)
+        def tile_cols(tiles):
+            return slice(tiles.start * P, tiles.stop * P)
+
+        def group(copy, grouped, raw, tiles):
             copy(
-                out=grouped[:, cols, :].rearrange("p (c i) t -> p c t i", i=RUN),
-                in_=raw[:, :, cols].rearrange("p t (c i) -> p c t i", i=RUN),
+                out=grouped[:, tile_cols(tiles), :].rearrange("p (c i) t -> p c t i", i=RUN),
+                in_=raw[:, :, tile_cols(tiles)].rearrange("p t (c i) -> p c t i", i=RUN),
             )
 
-        def quantise(codes, scales, grouped, tile):
-            cols = slice(tile * P, (tile + 1) * P)
+        def quantise(codes, scales, grouped, tiles):
             nc.vector.quantize_mx(
-                out=codes[:, cols].bitcast(FP8X4),
-                scales=scales[:, cols],
-                in_=grouped[:, cols, :].rearrange("p c t -> p (c t)"),
+                out=codes[:, tile_cols(tiles)].bitcast(FP8X4),
+                scales=scales[:, tile_cols(tiles)],
+                in_=grouped[:, tile_cols(tiles), :].rearrange("p c t -> p (c t)"),
             )
 
         ident = keep.tile([P, P], F32)
         masks.make_identity(nc, ident[:])
         one_col = keep.tile([P, 1], F32)
         nc.vector.memset(one_col[:], 1.0)
+        cap_col = keep.tile([P, 1], F32)
+        nc.vector.memset(cap_col[:], EXP_CAP)
 
         y_codes = keep.tile([P, ROWS], U32, align_bytes=64)
         y_scales = keep.tile([P, ROWS], U8, align_bytes=64)
@@ -126,16 +128,16 @@ def tile_deepgmm_pa_s_kernel(
 
             y_sb = early.tile([P, NT, Y_DIM], BF16)
             nc.sync.dma_start(out=y_sb[:], in_=Y.rearrange("(t p) k -> p t k", p=P))
-            for row, rows in (
-                (ROW_PHI_SIG, phi_sigs),
-                (ROW_PHI_MU, phi_mus),
-                (ROW_BE_SIG, be_sig.rearrange("(o d) -> o d", o=1)),
-                (ROW_BE_MU, be_mu.rearrange("(o d) -> o d", o=1)),
-            ):
-                nc.sync.dma_start(out=param_rows[row : row + rows.shape[0], :], in_=rows)
             wsig_raw = early.tile([P, PACK, X_DIM], BF16)
             wmu_raw = early.tile([P, PACK, X_DIM], BF16)
             load_weight(wsig_raw, We_sig)
+            for row, rows in (
+                (ROW_BE_SIG, be_sig.rearrange("(o d) -> o d", o=1)),
+                (ROW_PHI_SIG, phi_sigs),
+                (ROW_BE_MU, be_mu.rearrange("(o d) -> o d", o=1)),
+                (ROW_PHI_MU, phi_mus),
+            ):
+                nc.sync.dma_start(out=param_rows[row : row + rows.shape[0], :], in_=rows)
             load_weight(wmu_raw, We_mu)
             nc.sync.dma_start(out=logits[:], in_=phi_logits.partition_broadcast(P))
 
@@ -160,34 +162,42 @@ def tile_deepgmm_pa_s_kernel(
                 nc.tensor.transpose(
                     param_ps[:, dt, :], param_rows[:, dt * P : (dt + 1) * P], ident_bf[:]
                 )
-            nc.scalar.copy(out=params[:], in_=param_ps[:, :, 0:PARAM_ROWS])
-
             y_grouped = early.tile([P, ROWS, PACK], BF16, align_bytes=64)
-            for nt in range(NT):
-                nc.vector.tensor_copy(
+            for copy, nt in ((nc.vector.tensor_copy, 0), (nc.scalar.copy, 1)):
+                copy(
                     out=y_grouped[:].bitcast(F32)[:, nt * P : (nt + 1) * P, :],
                     in_=y_banks[nt][:].rearrange("p u n -> p n u"),
                 )
-            for nt in range(NT):
-                quantise(y_codes, y_scales, y_grouped, nt)
-
+            halves = (slice(0, DT // 2), slice(DT // 2, DT))
             wsig_grouped = early.tile([P, X_DIM, PACK], BF16, align_bytes=64)
-            group(nc.scalar.copy, wsig_grouped, wsig_raw, DT - 1)
-            group(nc.vector.tensor_copy, wsig_grouped, wsig_raw, 0)
-            for dt in range(DT):
-                if dt + 1 < DT - 1:
-                    group(nc.vector.tensor_copy, wsig_grouped, wsig_raw, dt + 1)
-                quantise(wsig_codes, wsig_scales, wsig_grouped, dt)
+            for copy, half in zip((nc.vector.tensor_copy, nc.scalar.copy), halves):
+                group(copy, wsig_grouped, wsig_raw, half)
+            quantise(y_codes, y_scales, y_grouped, slice(0, NT))
+            for half in halves:
+                quantise(wsig_codes, wsig_scales, wsig_grouped, half)
             sig_acc = []
             for dt in range(DT):
                 acc = psum.tile([P, ROWS], F32, tag="bank")
                 project(acc[:], wsig_codes, wsig_scales, dt)
                 sig_acc.append(acc)
 
+            nc.scalar.copy(out=params[:], in_=param_ps[:, :, 0:PARAM_ROWS])
+            cap_less_be = early.tile([P, 1], F32)
+            nc.scalar.activation(
+                out=cap_less_be[:], in_=param_ps[:, 0, ROW_BE_SIG : ROW_BE_SIG + 1],
+                func=ACT.Identity, scale=-1.0, bias=cap_col[:],
+            )
             cap_v = early.tile([P, DT, ROWS], F32)
             exp_v = early.tile([P, DT, ROWS], F32)
             log_v = early.tile([P, DT, ROWS], F32)
-            for dt in range(DT):
+            nc.scalar.activation(
+                out=cap_v[:, 0, :], in_=sig_acc[0][:], func=ACT.Relu,
+                scale=-1.0, bias=cap_less_be[:],
+            )
+            nc.scalar.activation(
+                out=exp_v[:, 0, :], in_=cap_v[:, 0, :], func=ACT.Exp, scale=-1.0, bias=cap_col[:]
+            )
+            for dt in range(1, DT):
                 nc.vector.tensor_scalar(
                     out=cap_v[:, dt, :], in0=sig_acc[dt][:],
                     scalar1=param(dt, ROW_BE_SIG), scalar2=EXP_CAP, op0=ALU.add, op1=ALU.min,
@@ -199,30 +209,39 @@ def tile_deepgmm_pa_s_kernel(
                 )
 
             wmu_grouped = early.tile([P, X_DIM, PACK], BF16, align_bytes=64)
-            group(nc.vector.tensor_copy, wmu_grouped, wmu_raw, 0)
-            for dt in range(DT):
-                if dt + 1 < DT:
-                    group(nc.vector.tensor_copy, wmu_grouped, wmu_raw, dt + 1)
-                quantise(wmu_codes, wmu_scales, wmu_grouped, dt)
+            for half in halves:
+                group(nc.vector.tensor_copy, wmu_grouped, wmu_raw, half)
+            for half in halves:
+                quantise(wmu_codes, wmu_scales, wmu_grouped, half)
             nc.vector.tensor_scalar(
                 out=floor_sig[:], in0=params[:, :, ROW_PHI_SIG : ROW_PHI_SIG + CLUSTERS],
                 scalar1=SIG_FLOOR, scalar2=None, op0=ALU.add,
             )
+            mu_acc = []
             for first in range(0, DT, TILES_PER_BANK):
-                mu_acc = psum.tile([P, TILES_PER_BANK, ROWS], F32, tag="bank")
+                bank = psum.tile([P, TILES_PER_BANK, ROWS], F32, tag="bank")
                 for j in range(TILES_PER_BANK):
-                    project(mu_acc[:, j, :], wmu_codes, wmu_scales, first + j)
-                for j in range(TILES_PER_BANK):
-                    nc.vector.tensor_scalar(
-                        out=muT[:, first + j, :], in0=mu_acc[:, j, :],
-                        scalar1=param(first + j, ROW_BE_MU), scalar2=None, op0=ALU.add,
-                    )
+                    project(bank[:, j, :], wmu_codes, wmu_scales, first + j)
+                    mu_acc.append(bank[:, j, :])
 
-            for dt in range(DT):
+            def enc_mu_tile(dt):
+                nc.vector.tensor_scalar(
+                    out=muT[:, dt, :], in0=mu_acc[dt],
+                    scalar1=param(dt, ROW_BE_MU), scalar2=None, op0=ALU.add,
+                )
+
+            def enc_sig_tile(dt):
                 nc.vector.scalar_tensor_tensor(
                     out=sigT[:, dt, :], in0=sig_acc[dt][:], scalar=param(dt, ROW_BE_SIG),
                     in1=log_v[:, dt, :], op0=ALU.add, op1=ALU.max,
                 )
+
+            for dt in range(DT):
+                enc_sig_tile(dt)
+                if dt == 1:
+                    enc_mu_tile(0)
+            for dt in range(1, DT):
+                enc_mu_tile(dt)
 
         work = ctx.enter_context(tc.tile_pool(name="work", bufs=3))
         outs = ctx.enter_context(tc.tile_pool(name="outs", bufs=2 * NT))
@@ -259,7 +278,7 @@ def tile_deepgmm_pa_s_kernel(
             square(nc.gpsimd, unit, diff)
 
         def scalar_square(block):
-            k, dt = divmod(VECTOR_CLUSTERS * DT + block, DT)
+            k, dt = divmod(VECTOR_UNITS * UNIT_TILES + block, DT)
             nc.scalar.activation(
                 out=dist2[:, k, dt, :], in_=muT[:, dt, :], func=ACT.Square,
                 scale=-1.0, bias=param(dt, ROW_PHI_MU + k),

@@ -38,23 +38,24 @@ ROW_BE_MU = 2 * CLUSTERS
 ROW_BE_SIG = 2 * CLUSTERS + 1
 PARAM_ROWS = 2 * CLUSTERS + 2
 
-VECTOR_UNITS = 21
-SCALAR_UNITS = 3
-UNIT_TILES = DT // 2
-UNITS_PER_CLUSTER = DT // UNIT_TILES
-GPSIMD_FIRST_UNIT = VECTOR_UNITS + SCALAR_UNITS
-ALL_UNITS = CLUSTERS * UNITS_PER_CLUSTER
-SCALAR_BLOCKS = SCALAR_UNITS * UNIT_TILES
-VECTOR_REST = 4
-VECTOR_LOOP_UNITS = VECTOR_UNITS - VECTOR_REST
-
-
-def d_on_partitions(k):
-    return k % 2 == 0
-
-
+SUMMED = (0, 3, 7, 10)
+ADDED = (1, 5, 8, 11, 14)
+PLAIN = tuple(k for k in range(CLUSTERS) if k not in SUMMED)
+GPSIMD_DIST2 = SUMMED[:2]
+VECTOR_DIST2 = SUMMED[2:]
+SUMMED_EVERY = 3
 FOLD_LAG = 3
 SUM_LAG = 5
+PRODUCT_LAG = 5
+ADD_LEAD = 2
+
+
+def second_order():
+    order = list(PLAIN)
+    for i, k in enumerate(SUMMED):
+        order = order[: SUMMED_EVERY * (i + 1)] + [k] + order[SUMMED_EVERY * (i + 1) :]
+    return order
+
 
 FLOPS = 2 * 2 * ROWS * Y_DIM * X_DIM
 
@@ -103,7 +104,9 @@ def tile_deepgmm_pa_s_kernel(
         logits = keep.tile([P, CLUSTERS], BF16)
         params = keep.tile([P, DT, PARAM_ROWS], F32)
         floor_sig = keep.tile([P, DT, CLUSTERS], F32)
-        muT = keep.tile([P, DT, ROWS], F32)
+        gap = keep.tile([P, DT, CLUSTERS], F32)
+        half_gap2 = keep.tile([P, DT, CLUSTERS], F32)
+        mmT = keep.tile([P, DT, ROWS], F32)
         sigT = keep.tile([P, DT, ROWS], F32)
 
         def param(dt, row):
@@ -217,158 +220,138 @@ def tile_deepgmm_pa_s_kernel(
                 out=floor_sig[:], in0=params[:, :, ROW_PHI_SIG : ROW_PHI_SIG + CLUSTERS],
                 scalar1=SIG_FLOOR, scalar2=None, op0=ALU.add,
             )
-            mu_acc = []
+            nc.vector.tensor_tensor(
+                out=gap[:], in0=params[:, :, ROW_PHI_MU : ROW_PHI_MU + CLUSTERS],
+                in1=params[:, :, ROW_BE_MU : ROW_BE_MU + 1].to_broadcast([P, DT, CLUSTERS]),
+                op=ALU.subtract,
+            )
+            mu_banks = []
             for first in range(0, DT, TILES_PER_BANK):
                 bank = psum.tile([P, TILES_PER_BANK, ROWS], F32, tag="bank")
                 for j in range(TILES_PER_BANK):
                     project(bank[:, j, :], wmu_codes, wmu_scales, first + j)
-                    mu_acc.append(bank[:, j, :])
+                mu_banks.append((slice(first, first + TILES_PER_BANK), bank))
+            nc.vector.scalar_tensor_tensor(
+                out=half_gap2[:], in0=gap[:], scalar=0.5, in1=gap[:], op0=ALU.mult, op1=ALU.mult
+            )
+            nc.vector.tensor_scalar(
+                out=gap[:], in0=gap[:], scalar1=-1.0, scalar2=None, op0=ALU.mult
+            )
 
-            def enc_mu_tile(dt):
-                nc.vector.tensor_scalar(
-                    out=muT[:, dt, :], in0=mu_acc[dt],
-                    scalar1=param(dt, ROW_BE_MU), scalar2=None, op0=ALU.add,
-                )
-
-            def enc_sig_tile(dt):
+            for dt in range(DT):
                 nc.vector.scalar_tensor_tensor(
                     out=sigT[:, dt, :], in0=sig_acc[dt][:], scalar=param(dt, ROW_BE_SIG),
                     in1=log_v[:, dt, :], op0=ALU.add, op1=ALU.max,
                 )
-
-            for dt in range(DT):
-                enc_sig_tile(dt)
-                if dt == 1:
-                    enc_mu_tile(0)
-            for dt in range(1, DT):
-                enc_mu_tile(dt)
+            for tiles, bank in mu_banks:
+                nc.vector.tensor_copy(out=mmT[:, tiles, :], in_=bank[:])
 
         work = ctx.enter_context(tc.tile_pool(name="work", bufs=3))
         outs = ctx.enter_context(tc.tile_pool(name="outs", bufs=2 * NT))
-        diffs = ctx.enter_context(tc.tile_pool(name="diffs", bufs=VECTOR_REST))
         ln_pool = ctx.enter_context(tc.tile_pool(name="ln_pool", bufs=CLUSTERS))
+        terms = ctx.enter_context(tc.tile_pool(name="terms", bufs=CLUSTERS))
 
-        dist2 = keep.tile([P, CLUSTERS, DT, ROWS], F32)
+        half_a2 = keep.tile([P, DT, ROWS], F32)
+        linear = {}
 
-        def vector_difference(unit):
-            k, part = divmod(unit, UNITS_PER_CLUSTER)
-            diff = diffs.tile([P, UNIT_TILES, ROWS], F32)
-            for j in range(UNIT_TILES):
-                dt = part * UNIT_TILES + j
+        def linear_term(k):
+            term = terms.tile([P, DT, ROWS], F32)
+            for dt in range(DT):
                 nc.vector.tensor_scalar(
-                    out=diff[:, j, :], in0=muT[:, dt, :],
-                    scalar1=param(dt, ROW_PHI_MU + k), scalar2=None, op0=ALU.subtract,
+                    out=term[:, dt, :], in0=mmT[:, dt, :],
+                    scalar1=gap[:, dt, k : k + 1], scalar2=half_gap2[:, dt, k : k + 1],
+                    op0=ALU.mult, op1=ALU.add,
                 )
-            return diff
+            linear[k] = term
 
-        def square(engine, unit, diff):
-            k, part = divmod(unit, UNITS_PER_CLUSTER)
-            tiles = slice(part * UNIT_TILES, (part + 1) * UNIT_TILES)
-            engine.tensor_tensor(out=dist2[:, k, tiles, :], in0=diff[:], in1=diff[:], op=ALU.mult)
+        def add_square(engine, k):
+            engine.tensor_tensor(out=linear[k][:], in0=linear[k][:], in1=half_a2[:], op=ALU.add)
 
-        def gpsimd_square(unit):
-            k, part = divmod(unit, UNITS_PER_CLUSTER)
-            diff = diffs.tile([P, UNIT_TILES, ROWS], F32)
-            for j in range(UNIT_TILES):
-                dt = part * UNIT_TILES + j
-                nc.gpsimd.tensor_scalar(
-                    out=diff[:, j, :], in0=muT[:, dt, :],
-                    scalar1=-1.0, scalar2=param(dt, ROW_PHI_MU + k), op0=ALU.mult, op1=ALU.add,
-                )
-            square(nc.gpsimd, unit, diff)
-
-        def scalar_square(block):
-            k, dt = divmod(VECTOR_UNITS * UNIT_TILES + block, DT)
-            nc.scalar.activation(
-                out=dist2[:, k, dt, :], in_=muT[:, dt, :], func=ACT.Square,
-                scale=-1.0, bias=param(dt, ROW_PHI_MU + k),
-            )
-
-        def rows_onto_partitions(src):
+        def rows_onto_partitions(nt, srcs):
+            rows = slice(nt * P, (nt + 1) * P)
             bank = psum.tile([P, X_DIM], F32, tag="bank")
             for dt in range(DT):
-                nc.tensor.transpose(bank[:, dt * P : (dt + 1) * P], src[:, dt, :], ident[:])
-            return bank
-
-        def std_rows(k, nt):
-            bank = psum.tile([P, X_DIM], F32, tag="bank")
-            for dt in range(DT):
-                for src, first in (
-                    (sigT[:, dt, nt * P : (nt + 1) * P], True),
-                    (floor_sig[:, dt, k : k + 1].to_broadcast([P, P]), False),
-                ):
+                for i, src in enumerate(srcs):
                     nc.tensor.matmul(
-                        bank[:, dt * P : (dt + 1) * P], lhsT=src, rhs=ident[:],
-                        start=first, stop=not first, is_transpose=True,
+                        bank[:, dt * P : (dt + 1) * P], lhsT=src[:, dt, rows], rhs=ident[:],
+                        start=i == 0, stop=i == len(srcs) - 1, is_transpose=True,
                     )
             return bank
 
-        ln_rows = {}
-        ln_cols = {}
-        ln_sum = keep.tile([P, NT, CLUSTERS], F32)
-        not_squared = []
+        def along_rows(values):
+            return values.unsqueeze(2).to_broadcast([P, DT, ROWS])
 
-        def vector_units(units):
-            for unit in units:
-                diff = vector_difference(unit)
-                if not_squared:
-                    square(nc.vector, *not_squared.pop())
-                not_squared.append((unit, diff))
-
-        folded = {}
-
-        def fold_d_tiles(k):
+        def fold_d_tiles(src):
             bank = psum.tile([P, NT, P], F32, tag="bank")
             for nt in range(NT):
                 for dt in range(DT):
                     nc.tensor.matmul(
-                        bank[:, nt, :], lhsT=ln_cols[k][:, dt, nt * P : (nt + 1) * P], rhs=ident[:],
+                        bank[:, nt, :], lhsT=src[:, dt, nt * P : (nt + 1) * P], rhs=ident[:],
                         start=dt == 0, stop=dt == DT - 1, is_transpose=True,
                     )
-            folded[k] = bank
+            return bank
 
-        def sum_folded(k):
-            nc.vector.tensor_reduce(
-                out=ln_sum[:, :, k], in_=folded[k][:], axis=AXIS.X, op=ALU.add
-            )
+        def sum_folded(out, bank):
+            nc.vector.tensor_reduce(out=out, in_=bank[:], axis=AXIS.X, op=ALU.add)
 
+        ln_std = {}
+        ln_sum = keep.tile([P, NT, CLUSTERS], F32)
+        std_tiles = {}
+
+        def add_phi_sigs(k):
+            stdT = work.tile([P, DT, ROWS], F32)
+            for dt in range(DT):
+                nc.vector.tensor_scalar(
+                    out=stdT[:, dt, :], in0=sigT[:, dt, :],
+                    scalar1=floor_sig[:, dt, k : k + 1], scalar2=None, op0=ALU.add,
+                )
+            std_tiles[k] = stdT
+
+        folded = {}
+        waiting = list(PLAIN + VECTOR_DIST2)
         for k in range(CLUSTERS):
-            if d_on_partitions(k):
-                ln_std = ln_pool.tile([P, DT, ROWS], F32)
+            if k in SUMMED:
+                ln = ln_pool.tile([P, DT, ROWS], F32)
                 for dt in range(DT):
                     nc.scalar.activation(
-                        out=ln_std[:, dt, :], in_=sigT[:, dt, :], func=ACT.Ln,
+                        out=ln[:, dt, :], in_=sigT[:, dt, :], func=ACT.Ln,
                         bias=floor_sig[:, dt, k : k + 1],
                     )
-                ln_cols[k] = ln_std
             else:
-                ln_std = ln_pool.tile([P, NT, X_DIM], F32)
+                ln = ln_pool.tile([P, NT, X_DIM], F32)
                 for nt in range(NT):
-                    std_bank = std_rows(k, nt)
+                    if k in ADDED:
+                        std_bank = rows_onto_partitions(
+                            nt, (sigT[:], along_rows(floor_sig[:, :, k]))
+                        )
+                    else:
+                        std_bank = rows_onto_partitions(nt, (std_tiles[k][:],))
                     nc.scalar.activation(
-                        out=ln_std[:, nt, :], in_=std_bank[:], func=ACT.Ln,
+                        out=ln[:, nt, :], in_=std_bank[:], func=ACT.Ln,
                         accum_out=ln_sum[:, nt, k : k + 1],
                     )
-                ln_rows[k] = ln_std
-            if k - FOLD_LAG in ln_cols:
-                fold_d_tiles(k - FOLD_LAG)
-            vector_units(
-                range(k * VECTOR_LOOP_UNITS // CLUSTERS, (k + 1) * VECTOR_LOOP_UNITS // CLUSTERS)
-            )
-            if k - SUM_LAG in folded:
-                sum_folded(k - SUM_LAG)
+            ln_std[k] = ln
+            if k - FOLD_LAG in SUMMED:
+                folded[k - FOLD_LAG] = fold_d_tiles(ln_std[k - FOLD_LAG][:])
+            if k + ADD_LEAD < CLUSTERS and k + ADD_LEAD not in SUMMED + ADDED:
+                add_phi_sigs(k + ADD_LEAD)
+            if k == 0:
+                nc.vector.scalar_tensor_tensor(
+                    out=half_a2[:], in0=mmT[:], scalar=0.5, in1=mmT[:], op0=ALU.mult, op1=ALU.mult
+                )
+            elif waiting:
+                linear_term(waiting.pop(0))
+            if k - SUM_LAG in SUMMED:
+                sum_folded(ln_sum[:, :, k - SUM_LAG], folded[k - SUM_LAG])
 
-        for k in range(CLUSTERS - FOLD_LAG, CLUSTERS):
-            if k in ln_cols:
-                fold_d_tiles(k)
-        vector_units(range(VECTOR_LOOP_UNITS, VECTOR_UNITS))
-        square(nc.vector, *not_squared.pop())
-        for k in range(CLUSTERS - SUM_LAG, CLUSTERS):
-            if k in folded:
-                sum_folded(k)
-        for unit in range(GPSIMD_FIRST_UNIT, ALL_UNITS):
-            gpsimd_square(unit)
-
+        for k in waiting:
+            linear_term(k)
+        for k in VECTOR_DIST2:
+            add_square(nc.vector, k)
+        for k in GPSIMD_DIST2:
+            linear_term(k)
+        for k in GPSIMD_DIST2:
+            add_square(nc.gpsimd, k)
         base = keep.tile([P, NT, CLUSTERS], F32)
         nc.vector.tensor_tensor(
             out=base[:], in0=logits[:].unsqueeze(1).to_broadcast([P, NT, CLUSTERS]), in1=ln_sum[:],
@@ -376,43 +359,48 @@ def tile_deepgmm_pa_s_kernel(
         )
 
         maha_sum = keep.tile([P, NT, CLUSTERS], F32)
-
-        def ln_of_rows(k):
-            if k in ln_rows:
-                return [(slice(0, NT), ln_rows[k][:])]
-            pieces = []
-            for nt in range(NT):
-                bank = rows_onto_partitions(ln_cols[k][:, :, nt * P : (nt + 1) * P])
-                pieces.append((nt, bank[:]))
-            return pieces
-
-        pieces = ln_of_rows(0)
-        for k in range(CLUSTERS):
-            inv_var = work.tile([P, NT, X_DIM], F32)
-            for rows, ln_std in pieces:
+        order = second_order()
+        for i, k in enumerate(order):
+            if k in SUMMED:
+                inv_var_cols = ln_pool.tile([P, DT, ROWS], F32, tag="inv_var_cols", bufs=len(SUMMED))
                 nc.scalar.activation(
-                    out=inv_var[:, rows, :], in_=ln_std, func=ACT.Exp, scale=-2.0
+                    out=inv_var_cols[:], in_=ln_std[k][:], func=ACT.Exp, scale=-2.0
                 )
-            if k < SCALAR_BLOCKS:
-                scalar_square(k)
-            if k + 1 < CLUSTERS:
-                pieces = ln_of_rows(k + 1)
-            for nt in range(NT):
-                dist2_bank = rows_onto_partitions(dist2[:, k, :, nt * P : (nt + 1) * P])
-                product = work.tile([P, X_DIM], F32)
-                nc.vector.scalar_tensor_tensor(
-                    out=product[:], in0=dist2_bank[:], scalar=0.5, in1=inv_var[:, nt, :],
-                    op0=ALU.mult, op1=ALU.mult, accum_out=maha_sum[:, nt, k : k + 1],
+                nc.gpsimd.tensor_tensor(
+                    out=linear[k][:], in0=linear[k][:], in1=inv_var_cols[:], op=ALU.mult
                 )
+            else:
+                inv_var = work.tile([P, NT, X_DIM], F32)
+                at_end = i in (0, CLUSTERS - 1)
+                for rows in [slice(nt, nt + 1) for nt in range(NT)] if at_end else [slice(0, NT)]:
+                    nc.scalar.activation(
+                        out=inv_var[:, rows, :], in_=ln_std[k][:, rows, :], func=ACT.Exp, scale=-2.0
+                    )
+                for nt in range(NT):
+                    dist2_bank = rows_onto_partitions(nt, (half_a2[:], linear[k][:]))
+                    product = work.tile([P, X_DIM], F32)
+                    nc.vector.scalar_tensor_tensor(
+                        out=product[:], in0=dist2_bank[:], scalar=1.0, in1=inv_var[:, nt, :],
+                        op0=ALU.mult, op1=ALU.mult, accum_out=maha_sum[:, nt, k : k + 1],
+                    )
+            for j, done in enumerate(order[: i + 1]):
+                if done in SUMMED and i == min(j + PRODUCT_LAG, CLUSTERS - 1):
+                    sum_folded(maha_sum[:, :, done], fold_d_tiles(linear[done][:]))
 
-        def store_rows(copy, dram, src):
+        def store_rows(dram, banks, copy):
             for nt in range(NT):
-                bank = rows_onto_partitions(src[:, :, nt * P : (nt + 1) * P])
                 rows_sb = outs.tile([P, X_DIM], F32)
-                copy(rows_sb[:], bank[:])
+                copy(rows_sb[:], banks[nt][:])
                 nc.sync.dma_start(out=dram[nt * P : (nt + 1) * P, :], in_=rows_sb[:])
 
-        store_rows(lambda out, in_: nc.scalar.copy(out=out, in_=in_), out_0, muT)
+        store_rows(
+            out_0,
+            [
+                rows_onto_partitions(nt, (mmT[:], along_rows(params[:, :, ROW_BE_MU])))
+                for nt in range(NT)
+            ],
+            lambda out, in_: nc.scalar.copy(out=out, in_=in_),
+        )
 
         neg_z = keep.tile([P, NT, CLUSTERS], F32)
         nc.vector.tensor_tensor(out=neg_z[:], in0=maha_sum[:], in1=base[:], op=ALU.subtract)
@@ -433,9 +421,9 @@ def tile_deepgmm_pa_s_kernel(
             op=ALU.subtract,
         )
         store_rows(
-            lambda out, in_: nc.vector.tensor_scalar_add(out=out, in0=in_, scalar1=SIG_FLOOR),
             out_1,
-            sigT,
+            [rows_onto_partitions(nt, (sigT[:],)) for nt in range(NT)],
+            lambda out, in_: nc.vector.tensor_scalar_add(out=out, in0=in_, scalar1=SIG_FLOOR),
         )
         z_log_probs = keep.tile([P, NT, CLUSTERS], F32)
         nc.vector.tensor_tensor(

@@ -41,8 +41,8 @@ PARAM_ROWS = 2 * CLUSTERS + 2
 SUMMED = (0, 3, 7, 10)
 ADDED = (1, 5, 8, 11, 14)
 PLAIN = tuple(k for k in range(CLUSTERS) if k not in SUMMED)
-GPSIMD_DIST2 = SUMMED[:2]
-VECTOR_DIST2 = SUMMED[2:]
+GPSIMD_DIST2 = SUMMED[:-1]
+VECTOR_DIST2 = (SUMMED[-1], PLAIN[-1])
 SUMMED_EVERY = 3
 FOLD_LAG = 3
 SUM_LAG = 5
@@ -308,7 +308,7 @@ def tile_deepgmm_pa_s_kernel(
             std_tiles[k] = stdT
 
         folded = {}
-        waiting = list(PLAIN + VECTOR_DIST2)
+        waiting = list(PLAIN + SUMMED[-1:])
         for k in range(CLUSTERS):
             if k in SUMMED:
                 ln = ln_pool.tile([P, DT, ROWS], F32)
@@ -348,7 +348,7 @@ def tile_deepgmm_pa_s_kernel(
             linear_term(k)
         for k in VECTOR_DIST2:
             add_square(nc.vector, k)
-        for k in GPSIMD_DIST2:
+        for k in reversed(GPSIMD_DIST2):
             linear_term(k)
         for k in GPSIMD_DIST2:
             add_square(nc.gpsimd, k)
@@ -359,7 +359,16 @@ def tile_deepgmm_pa_s_kernel(
         )
 
         maha_sum = keep.tile([P, NT, CLUSTERS], F32)
+
+        def sum_product(k):
+            sum_folded(maha_sum[:, :, k], fold_d_tiles(linear[k][:]))
+
+        def dist2_banks(k):
+            dist2 = (linear[k][:],) if k in VECTOR_DIST2 else (half_a2[:], linear[k][:])
+            return [rows_onto_partitions(nt, dist2) for nt in range(NT)]
+
         order = second_order()
+        next_banks = [dist2_banks(PLAIN[0])]
         for i, k in enumerate(order):
             if k in SUMMED:
                 inv_var_cols = ln_pool.tile([P, DT, ROWS], F32, tag="inv_var_cols", bufs=len(SUMMED))
@@ -376,16 +385,17 @@ def tile_deepgmm_pa_s_kernel(
                     nc.scalar.activation(
                         out=inv_var[:, rows, :], in_=ln_std[k][:, rows, :], func=ACT.Exp, scale=-2.0
                     )
+                banks, next_banks = next_banks, [
+                    dist2_banks(ahead) for ahead in PLAIN[PLAIN.index(k) + 1 :][:1]
+                ]
                 for nt in range(NT):
-                    dist2_bank = rows_onto_partitions(nt, (half_a2[:], linear[k][:]))
                     product = work.tile([P, X_DIM], F32)
                     nc.vector.scalar_tensor_tensor(
-                        out=product[:], in0=dist2_bank[:], scalar=1.0, in1=inv_var[:, nt, :],
+                        out=product[:], in0=banks[0][nt][:], scalar=1.0, in1=inv_var[:, nt, :],
                         op0=ALU.mult, op1=ALU.mult, accum_out=maha_sum[:, nt, k : k + 1],
                     )
-            for j, done in enumerate(order[: i + 1]):
-                if done in SUMMED and i == min(j + PRODUCT_LAG, CLUSTERS - 1):
-                    sum_folded(maha_sum[:, :, done], fold_d_tiles(linear[done][:]))
+            if i >= PRODUCT_LAG and order[i - PRODUCT_LAG] in SUMMED:
+                sum_product(order[i - PRODUCT_LAG])
 
         def store_rows(dram, banks, copy):
             for nt in range(NT):
@@ -401,6 +411,9 @@ def tile_deepgmm_pa_s_kernel(
             ],
             lambda out, in_: nc.scalar.copy(out=out, in_=in_),
         )
+        for k in order[CLUSTERS - PRODUCT_LAG :]:
+            if k in SUMMED:
+                sum_product(k)
 
         neg_z = keep.tile([P, NT, CLUSTERS], F32)
         nc.vector.tensor_tensor(out=neg_z[:], in0=maha_sum[:], in1=base[:], op=ALU.subtract)

from contextlib import ExitStack

import concourse.masks as masks
import concourse.mybir as mybir

F32 = mybir.dt.float32
BF16 = mybir.dt.bfloat16
U32 = mybir.dt.uint32
U8 = mybir.dt.uint8
FP8X4 = mybir.dt.float8_e4m3fn_x4
ACT = mybir.ActivationFunctionType
ALU = mybir.AluOpType
AXIS = mybir.AxisListType

P = 128
PSUM_BANKS = 8

ROWS = 256
Y_DIM = 512
X_DIM = 512
CLUSTERS = 16
SIG_FLOOR = 1e-3
EXP_CAP = 30.0
QUADRANT = 32
NT = ROWS // P
DT = X_DIM // P

PACK = 4
PAIR = 2
WORDS = PACK // PAIR
assert Y_DIM == P * PACK
TILES_PER_BANK = 2
RUN = 4

ROW_PHI_MU = 0
ROW_PHI_SIG = CLUSTERS
ROW_BE_MU = 2 * CLUSTERS
ROW_BE_SIG = 2 * CLUSTERS + 1
PARAM_ROWS = 2 * CLUSTERS + 2

SUMMED = (0, 3, 7, 10)
ADDED = (1, 5, 8, 11, 14)
PLAIN = tuple(k for k in range(CLUSTERS) if k not in SUMMED)
GPSIMD_DIST2 = SUMMED[:-1]
VECTOR_DIST2 = (SUMMED[-1], PLAIN[-1])
SUMMED_EVERY = 3
FOLD_LAG = 3
SUM_LAG = 5
PRODUCT_LAG = 5
ADD_LEAD = 2


def second_order():
    order = list(PLAIN)
    for i, k in enumerate(SUMMED):
        order = order[: SUMMED_EVERY * (i + 1)] + [k] + order[SUMMED_EVERY * (i + 1) :]
    return order


FLOPS = 2 * 2 * ROWS * Y_DIM * X_DIM


def tile_deepgmm_pa_s_kernel(
    tc, Y, We_mu, be_mu, We_sig, be_sig, phi_mus, phi_sigs, phi_logits, out_0, out_1, out_2
):
    nc = tc.nc
    with ExitStack() as ctx:
        keep = ctx.enter_context(tc.tile_pool(name="keep", bufs=1))
        psum = ctx.enter_context(tc.psum_pool(name="psum", bufs=PSUM_BANKS))
        ctx.enter_context(tc.manual_schedule())

        def load_weight(raw, w):
            nc.sync.dma_start(out=raw[:], in_=w.rearrange("(p t) c -> p t c", t=PACK))

        def tile_cols(tiles):
            return slice(tiles.start * P, tiles.stop * P)

        def group(copy, grouped, raw, tiles):
            copy(
                out=grouped[:, tile_cols(tiles), :].rearrange("p (c i) t -> p c t i", i=RUN),
                in_=raw[:, :, tile_cols(tiles)].rearrange("p t (c i) -> p c t i", i=RUN),
            )

        def quantise(codes, scales, grouped, tiles):
            nc.vector.quantize_mx(
                out=codes[:, tile_cols(tiles)].bitcast(FP8X4),
                scales=scales[:, tile_cols(tiles)],
                in_=grouped[:, tile_cols(tiles), :].rearrange("p c t -> p (c t)"),
            )

        ident = keep.tile([P, P], F32)
        masks.make_identity(nc, ident[:])
        one_col = keep.tile([P, 1], F32)
        nc.vector.memset(one_col[:], 1.0)
        cap_col = keep.tile([P, 1], F32)
        nc.vector.memset(cap_col[:], EXP_CAP)

        y_codes = keep.tile([P, ROWS], U32, align_bytes=64)
        y_scales = keep.tile([P, ROWS], U8, align_bytes=64)
        wsig_codes = keep.tile([P, X_DIM], U32, align_bytes=64)
        wsig_scales = keep.tile([P, X_DIM], U8, align_bytes=64)
        wmu_codes = keep.tile([P, X_DIM], U32, align_bytes=64)
        wmu_scales = keep.tile([P, X_DIM], U8, align_bytes=64)
        logits = keep.tile([P, CLUSTERS], BF16)
        params = keep.tile([P, DT, PARAM_ROWS], F32)
        floor_sig = keep.tile([P, DT, CLUSTERS], F32)
        gap = keep.tile([P, DT, CLUSTERS], F32)
        half_gap2 = keep.tile([P, DT, CLUSTERS], F32)
        mmT = keep.tile([P, DT, ROWS], F32)
        sigT = keep.tile([P, DT, ROWS], F32)

        def param(dt, row):
            return params[:, dt, row : row + 1]

        def project(out, w_codes, w_scales, dt):
            cols = slice(dt * P, (dt + 1) * P)
            nc.tensor.matmul_mx(
                out=out,
                lhsT=w_codes[:, cols].bitcast(FP8X4),
                lhsT_scale=w_scales[:, cols],
                rhs=y_codes[:].bitcast(FP8X4),
                rhs_scale=y_scales[:],
                start=True,
                stop=True,
            )

        with tc.tile_pool(name="early", bufs=1) as early:
            param_rows = early.tile([P, X_DIM], BF16)
            nc.vector.memset(param_rows[QUADRANT : 2 * QUADRANT, :], 0.0)
            nc.vector.memset(param_rows[2 * QUADRANT :, :], 0.0)

            y_sb = early.tile([P, NT, Y_DIM], BF16)
            nc.sync.dma_start(out=y_sb[:], in_=Y.rearrange("(t p) k -> p t k", p=P))
            wsig_raw = early.tile([P, PACK, X_DIM], BF16)
            wmu_raw = early.tile([P, PACK, X_DIM], BF16)
            load_weight(wsig_raw, We_sig)
            for row, rows in (
                (ROW_BE_SIG, be_sig.rearrange("(o d) -> o d", o=1)),
                (ROW_PHI_SIG, phi_sigs),
                (ROW_BE_MU, be_mu.rearrange("(o d) -> o d", o=1)),
                (ROW_PHI_MU, phi_mus),
            ):
                nc.sync.dma_start(out=param_rows[row : row + rows.shape[0], :], in_=rows)
            load_weight(wmu_raw, We_mu)
            nc.sync.dma_start(out=logits[:], in_=phi_logits.partition_broadcast(P))

            warm = keep.tile([P, 1], F32)
            nc.scalar.activation(out=warm[:], in_=one_col[:], func=ACT.Exp)

            ident_bf = early.tile([P, P], BF16)
            nc.vector.tensor_copy(out=ident_bf[:], in_=ident[:])

            y_words = y_sb[:].bitcast(F32)
            y_banks = []
            for nt in range(NT):
                yT_ps = psum.tile([P, WORDS, P], F32, tag="bank")
                for u in range(WORDS):
                    nc.tensor.transpose(
                        yT_ps[:, u, :], y_words[:, nt, u : WORDS * P : WORDS], ident[:]
                    )
                y_banks.append(yT_ps)

            param_ps = psum.tile([P, DT, P], BF16, tag="bank")
            for dt in range(DT):
                nc.tensor.transpose(
                    param_ps[:, dt, :], param_rows[:, dt * P : (dt + 1) * P], ident_bf[:]
                )
            y_grouped = early.tile([P, ROWS, PACK], BF16, align_bytes=64)
            for copy, nt in ((nc.vector.tensor_copy, 0), (nc.scalar.copy, 1)):
                copy(
                    out=y_grouped[:].bitcast(F32)[:, nt * P : (nt + 1) * P, :],
                    in_=y_banks[nt][:].rearrange("p u n -> p n u"),
                )
            halves = (slice(0, DT // 2), slice(DT // 2, DT))
            wsig_grouped = early.tile([P, X_DIM, PACK], BF16, align_bytes=64)
            for copy, half in zip((nc.vector.tensor_copy, nc.scalar.copy), halves):
                group(copy, wsig_grouped, wsig_raw, half)
            quantise(y_codes, y_scales, y_grouped, slice(0, NT))
            for half in halves:
                quantise(wsig_codes, wsig_scales, wsig_grouped, half)
            sig_acc = []
            for dt in range(DT):
                acc = psum.tile([P, ROWS], F32, tag="bank")
                project(acc[:], wsig_codes, wsig_scales, dt)
                sig_acc.append(acc)

            nc.scalar.copy(out=params[:], in_=param_ps[:, :, 0:PARAM_ROWS])
            cap_less_be = early.tile([P, 1], F32)
            nc.scalar.activation(
                out=cap_less_be[:], in_=param_ps[:, 0, ROW_BE_SIG : ROW_BE_SIG + 1],
                func=ACT.Identity, scale=-1.0, bias=cap_col[:],
            )
            cap_v = early.tile([P, DT, ROWS], F32)
            exp_v = early.tile([P, DT, ROWS], F32)
            log_v = early.tile([P, DT, ROWS], F32)
            nc.scalar.activation(
                out=cap_v[:, 0, :], in_=sig_acc[0][:], func=ACT.Relu,
                scale=-1.0, bias=cap_less_be[:],
            )
            nc.scalar.activation(
                out=exp_v[:, 0, :], in_=cap_v[:, 0, :], func=ACT.Exp, scale=-1.0, bias=cap_col[:]
            )
            for dt in range(1, DT):
                nc.vector.tensor_scalar(
                    out=cap_v[:, dt, :], in0=sig_acc[dt][:],
                    scalar1=param(dt, ROW_BE_SIG), scalar2=EXP_CAP, op0=ALU.add, op1=ALU.min,
                )
                nc.scalar.activation(out=exp_v[:, dt, :], in_=cap_v[:, dt, :], func=ACT.Exp)
            for dt in range(DT):
                nc.scalar.activation(
                    out=log_v[:, dt, :], in_=exp_v[:, dt, :], func=ACT.Ln, bias=one_col[:]
                )

            wmu_grouped = early.tile([P, X_DIM, PACK], BF16, align_bytes=64)
            for half in halves:
                group(nc.vector.tensor_copy, wmu_grouped, wmu_raw, half)
            for half in halves:
                quantise(wmu_codes, wmu_scales, wmu_grouped, half)
            nc.vector.tensor_scalar(
                out=floor_sig[:], in0=params[:, :, ROW_PHI_SIG : ROW_PHI_SIG + CLUSTERS],
                scalar1=SIG_FLOOR, scalar2=None, op0=ALU.add,
            )
            nc.vector.tensor_tensor(
                out=gap[:], in0=params[:, :, ROW_PHI_MU : ROW_PHI_MU + CLUSTERS],
                in1=params[:, :, ROW_BE_MU : ROW_BE_MU + 1].to_broadcast([P, DT, CLUSTERS]),
                op=ALU.subtract,
            )
            mu_banks = []
            for first in range(0, DT, TILES_PER_BANK):
                bank = psum.tile([P, TILES_PER_BANK, ROWS], F32, tag="bank")
                for j in range(TILES_PER_BANK):
                    project(bank[:, j, :], wmu_codes, wmu_scales, first + j)
                mu_banks.append((slice(first, first + TILES_PER_BANK), bank))
            nc.vector.scalar_tensor_tensor(
                out=half_gap2[:], in0=gap[:], scalar=0.5, in1=gap[:], op0=ALU.mult, op1=ALU.mult
            )
            nc.vector.tensor_scalar(
                out=gap[:], in0=gap[:], scalar1=-1.0, scalar2=None, op0=ALU.mult
            )

            for dt in range(DT):
                nc.vector.scalar_tensor_tensor(
                    out=sigT[:, dt, :], in0=sig_acc[dt][:], scalar=param(dt, ROW_BE_SIG),
                    in1=log_v[:, dt, :], op0=ALU.add, op1=ALU.max,
                )
            for tiles, bank in mu_banks:
                nc.vector.tensor_copy(out=mmT[:, tiles, :], in_=bank[:])

        work = ctx.enter_context(tc.tile_pool(name="work", bufs=3))
        outs = ctx.enter_context(tc.tile_pool(name="outs", bufs=2 * NT))
        ln_pool = ctx.enter_context(tc.tile_pool(name="ln_pool", bufs=CLUSTERS))
        terms = ctx.enter_context(tc.tile_pool(name="terms", bufs=CLUSTERS))

        half_a2 = keep.tile([P, DT, ROWS], F32)
        linear = {}

        def linear_term(k):
            term = terms.tile([P, DT, ROWS], F32)
            for dt in range(DT):
                nc.vector.tensor_scalar(
                    out=term[:, dt, :], in0=mmT[:, dt, :],
                    scalar1=gap[:, dt, k : k + 1], scalar2=half_gap2[:, dt, k : k + 1],
                    op0=ALU.mult, op1=ALU.add,
                )
            linear[k] = term

        def add_square(engine, k):
            engine.tensor_tensor(out=linear[k][:], in0=linear[k][:], in1=half_a2[:], op=ALU.add)

        def rows_onto_partitions(nt, srcs):
            rows = slice(nt * P, (nt + 1) * P)
            bank = psum.tile([P, X_DIM], F32, tag="bank")
            for dt in range(DT):
                for i, src in enumerate(srcs):
                    nc.tensor.matmul(
                        bank[:, dt * P : (dt + 1) * P], lhsT=src[:, dt, rows], rhs=ident[:],
                        start=i == 0, stop=i == len(srcs) - 1, is_transpose=True,
                    )
            return bank

        def along_rows(values):
            return values.unsqueeze(2).to_broadcast([P, DT, ROWS])

        def fold_d_tiles(src):
            bank = psum.tile([P, NT, P], F32, tag="bank")
            for nt in range(NT):
                for dt in range(DT):
                    nc.tensor.matmul(
                        bank[:, nt, :], lhsT=src[:, dt, nt * P : (nt + 1) * P], rhs=ident[:],
                        start=dt == 0, stop=dt == DT - 1, is_transpose=True,
                    )
            return bank

        def sum_folded(out, bank):
            nc.vector.tensor_reduce(out=out, in_=bank[:], axis=AXIS.X, op=ALU.add)

        ln_std = {}
        ln_sum = keep.tile([P, NT, CLUSTERS], F32)
        std_tiles = {}

        def add_phi_sigs(k):
            stdT = work.tile([P, DT, ROWS], F32)
            for dt in range(DT):
                nc.vector.tensor_scalar(
                    out=stdT[:, dt, :], in0=sigT[:, dt, :],
                    scalar1=floor_sig[:, dt, k : k + 1], scalar2=None, op0=ALU.add,
                )
            std_tiles[k] = stdT

        folded = {}
        waiting = list(PLAIN + SUMMED[-1:])
        for k in range(CLUSTERS):
            if k in SUMMED:
                ln = ln_pool.tile([P, DT, ROWS], F32)
                for dt in range(DT):
                    nc.scalar.activation(
                        out=ln[:, dt, :], in_=sigT[:, dt, :], func=ACT.Ln,
                        bias=floor_sig[:, dt, k : k + 1],
                    )
            else:
                ln = ln_pool.tile([P, NT, X_DIM], F32)
                for nt in range(NT):
                    if k in ADDED:
                        std_bank = rows_onto_partitions(
                            nt, (sigT[:], along_rows(floor_sig[:, :, k]))
                        )
                    else:
                        std_bank = rows_onto_partitions(nt, (std_tiles[k][:],))
                    nc.scalar.activation(
                        out=ln[:, nt, :], in_=std_bank[:], func=ACT.Ln,
                        accum_out=ln_sum[:, nt, k : k + 1],
                    )
            ln_std[k] = ln
            if k - FOLD_LAG in SUMMED:
                folded[k - FOLD_LAG] = fold_d_tiles(ln_std[k - FOLD_LAG][:])
            if k + ADD_LEAD < CLUSTERS and k + ADD_LEAD not in SUMMED + ADDED:
                add_phi_sigs(k + ADD_LEAD)
            if k == 0:
                nc.vector.scalar_tensor_tensor(
                    out=half_a2[:], in0=mmT[:], scalar=0.5, in1=mmT[:], op0=ALU.mult, op1=ALU.mult
                )
            elif waiting:
                linear_term(waiting.pop(0))
            if k - SUM_LAG in SUMMED:
                sum_folded(ln_sum[:, :, k - SUM_LAG], folded[k - SUM_LAG])

        for k in waiting:
            linear_term(k)
        for k in VECTOR_DIST2:
            add_square(nc.vector, k)
        for k in reversed(GPSIMD_DIST2):
            linear_term(k)
        for k in GPSIMD_DIST2:
            add_square(nc.gpsimd, k)
        base = keep.tile([P, NT, CLUSTERS], F32)
        nc.vector.tensor_tensor(
            out=base[:], in0=logits[:].unsqueeze(1).to_broadcast([P, NT, CLUSTERS]), in1=ln_sum[:],
            op=ALU.subtract,
        )

        maha_sum = keep.tile([P, NT, CLUSTERS], F32)

        def sum_product(k):
            sum_folded(maha_sum[:, :, k], fold_d_tiles(linear[k][:]))

        def dist2_banks(k):
            dist2 = (linear[k][:],) if k in VECTOR_DIST2 else (half_a2[:], linear[k][:])
            return [rows_onto_partitions(nt, dist2) for nt in range(NT)]

        order = second_order()
        next_banks = [dist2_banks(PLAIN[0])]
        for i, k in enumerate(order):
            if k in SUMMED:
                inv_var_cols = ln_pool.tile([P, DT, ROWS], F32, tag="inv_var_cols", bufs=len(SUMMED))
                nc.scalar.activation(
                    out=inv_var_cols[:], in_=ln_std[k][:], func=ACT.Exp, scale=-2.0
                )
                nc.gpsimd.tensor_tensor(
                    out=linear[k][:], in0=linear[k][:], in1=inv_var_cols[:], op=ALU.mult
                )
            else:
                inv_var = work.tile([P, NT, X_DIM], F32)
                at_end = i in (0, CLUSTERS - 1)
                for rows in [slice(nt, nt + 1) for nt in range(NT)] if at_end else [slice(0, NT)]:
                    nc.scalar.activation(
                        out=inv_var[:, rows, :], in_=ln_std[k][:, rows, :], func=ACT.Exp, scale=-2.0
                    )
                banks, next_banks = next_banks, [
                    dist2_banks(ahead) for ahead in PLAIN[PLAIN.index(k) + 1 :][:1]
                ]
                for nt in range(NT):
                    product = work.tile([P, X_DIM], F32)
                    nc.vector.scalar_tensor_tensor(
                        out=product[:], in0=banks[0][nt][:], scalar=1.0, in1=inv_var[:, nt, :],
                        op0=ALU.mult, op1=ALU.mult, accum_out=maha_sum[:, nt, k : k + 1],
                    )
            if i >= PRODUCT_LAG and order[i - PRODUCT_LAG] in SUMMED:
                sum_product(order[i - PRODUCT_LAG])

        def store_rows(dram, banks, copy):
            for nt in range(NT):
                rows_sb = outs.tile([P, X_DIM], F32)
                copy(rows_sb[:], banks[nt][:])
                nc.sync.dma_start(out=dram[nt * P : (nt + 1) * P, :], in_=rows_sb[:])

        store_rows(
            out_0,
            [
                rows_onto_partitions(nt, (mmT[:], along_rows(params[:, :, ROW_BE_MU])))
                for nt in range(NT)
            ],
            lambda out, in_: nc.scalar.copy(out=out, in_=in_),
        )
        for k in order[CLUSTERS - PRODUCT_LAG :]:
            if k in SUMMED:
                sum_product(k)

        neg_z = keep.tile([P, NT, CLUSTERS], F32)
        nc.vector.tensor_tensor(out=neg_z[:], in0=maha_sum[:], in1=base[:], op=ALU.subtract)
        low = keep.tile([P, NT], F32)
        nc.vector.tensor_reduce(out=low[:], in_=neg_z[:], axis=AXIS.X, op=ALU.min)
        exp_z = keep.tile([P, NT, CLUSTERS], F32)
        exp_sum = keep.tile([P, NT], F32)
        for nt in range(NT):
            nc.scalar.activation(
                out=exp_z[:, nt, :], in_=neg_z[:, nt, :], func=ACT.Exp,
                scale=-1.0, bias=low[:, nt : nt + 1], accum_out=exp_sum[:, nt : nt + 1],
            )
        log_sum = keep.tile([P, NT], F32)
        nc.scalar.activation(out=log_sum[:], in_=exp_sum[:], func=ACT.Ln)
        shifted = keep.tile([P, NT, CLUSTERS], F32)
        nc.vector.tensor_tensor(
            out=shifted[:], in0=low[:].unsqueeze(2).to_broadcast([P, NT, CLUSTERS]), in1=neg_z[:],
            op=ALU.subtract,
        )
        store_rows(
            out_1,
            [rows_onto_partitions(nt, (sigT[:],)) for nt in range(NT)],
            lambda out, in_: nc.vector.tensor_scalar_add(out=out, in0=in_, scalar1=SIG_FLOOR),
        )
        z_log_probs = keep.tile([P, NT, CLUSTERS], F32)
        nc.vector.tensor_tensor(
            out=z_log_probs[:], in0=shifted[:],
            in1=log_sum[:].unsqueeze(2).to_broadcast([P, NT, CLUSTERS]), op=ALU.subtract,
        )
        nc.sync.dma_start(out=out_2.rearrange("(t p) k -> p t k", p=P), in_=z_log_probs[:])
